import numpy as np
import ml_dtypes


def mxq(x, axis, fmt="e4m3"):
    dtype, down = {"e4m3": (ml_dtypes.float8_e4m3fn, 7), "e5m2": (ml_dtypes.float8_e5m2, 14)}[fmt]
    v = np.moveaxis(np.asarray(x, np.float32).astype(ml_dtypes.bfloat16).astype(np.float64), axis, -1)
    blocks = v.reshape(v.shape[:-1] + (-1, 32))
    amax = np.abs(blocks).max(-1, keepdims=True)
    byte = np.maximum(np.where(amax > 0, np.frexp(amax)[1] - 1 + 127, 0) - down, 1)
    scale = np.exp2(byte - 127.0)
    codes = (blocks / scale).astype(np.float32).astype(dtype).astype(np.float64)
    return np.moveaxis((codes * scale).reshape(v.shape), -1, axis)


WIDE = False


def mx_kscale(k):
    if not WIDE:
        return np.ones(k)
    levels = np.array([10, -10, 5, -5, 0])
    a = np.random.permutation(np.resize(levels, k // 512 * 4)).reshape(k // 512, 4)
    idx = np.arange(k)
    return np.exp2(a[idx // 512, idx % 128 // 32])


BF16 = ml_dtypes.bfloat16


def bf(x):
    return np.asarray(x, np.float32).astype(BF16)


def f64(x):
    return np.asarray(x).astype(np.float64)


B, NT, N, C, DV, TM = 4, 128, 1024, 1024, 256, 128


def softmax(s):
    e = np.exp(s - s.max(-1, keepdims=True))
    return e / e.sum(-1, keepdims=True)


def setup_inputs():
    s = mx_kscale(C)
    q = np.random.standard_normal((B, 1, C)) + np.random.standard_normal((B, NT, C))
    k = bf(np.random.standard_normal((B, N, C)) * 1.4)
    ki = bf(np.random.standard_normal((B, N, C)) * 1.4)
    ki[-1] = k[-1]
    return {'q': bf(q), 'k': k, 'ki': ki,
            'xs': bf(np.random.standard_normal((B, N, C)) * s),
            'xis': bf(np.random.standard_normal((B, N, C)) * s),
            'Wv': bf(np.random.standard_normal((C, DV)) * 1.8 / np.sqrt(C) / s[:, None])}


def reference(q, k, ki, xs, xis, Wv):
    scale = C ** -0.5
    aw = softmax(f64(q) @ f64(k).transpose(0, 2, 1) * scale)
    awi = softmax(f64(q) @ f64(ki).transpose(0, 2, 1) * scale)
    D = aw - awi
    ones_cnt = np.where(D > 0, 1.0, 0.0).sum(axis=1)
    half_cnt = np.where(D == 0, 1.0, 0.0).sum(axis=1)
    rgb_ratio = (ones_cnt / NT)[..., None]
    eq_ratio = (half_cnt / NT)[..., None]
    tir_ratio = 1.0 - rgb_ratio - eq_ratio
    wv = mxq(f64(Wv), 0, 'e4m3')
    v = mxq(f64(xs), 2, 'e4m3') @ wv
    vi = mxq(f64(xis), 2, 'e4m3') @ wv
    return v * (rgb_ratio + eq_ratio) + vi * (tir_ratio + eq_ratio)

@@ -1,0 +1,372 @@
+from contextlib import ExitStack
+
+import concourse.bass as bass
+import concourse.masks as masks
+import concourse.mybir as mybir
+import concourse.tile as tile
+
+F32 = mybir.dt.float32
+BF16 = mybir.dt.bfloat16
+U32 = mybir.dt.uint32
+U8 = mybir.dt.uint8
+FP8X4 = mybir.dt.float8_e4m3fn_x4
+ALU = mybir.AluOpType
+ACTF = mybir.ActivationFunctionType
+AX = mybir.AxisListType
+
+B, NT, N, C, DV = 4, 128, 1024, 1024, 256
+P = 128
+FLOPS = 2 * 2 * B * NT * N * C + 2 * 2 * B * N * C * DV
+SCALE = 1.0 / 32.0
+
+MANUAL = True
+LEAD = 6
+NB = 8
+AHEAD = 7
+EVAC = ("s", "s", "v", "s")
+
+
+def tile_crossattention_for_fusion_temporal_pa_t_kernel(tc, q, k, ki, xs, xis, Wv, out):
+    nc = tc.nc
+    with ExitStack() as ctx:
+        if MANUAL:
+            ctx.enter_context(tc.manual_schedule())
+        const = ctx.enter_context(tc.tile_pool(name="const", bufs=1))
+        rawp = ctx.enter_context(tc.tile_pool(name="rawp", bufs=NB))
+        qp = ctx.enter_context(tc.tile_pool(name="qp", bufs=2))
+        ktp = ctx.enter_context(tc.tile_pool(name="ktp", bufs=4))
+        grpp = ctx.enter_context(tc.tile_pool(name="grpp", bufs=3))
+        codp = ctx.enter_context(tc.tile_pool(name="codp", bufs=4))
+        ep = ctx.enter_context(tc.tile_pool(name="ep", bufs=2))
+        stp = ctx.enter_context(tc.tile_pool(name="stp", bufs=4))
+        abp = ctx.enter_context(tc.tile_pool(name="abp", bufs=3))
+        outp = ctx.enter_context(tc.tile_pool(name="outp", bufs=3))
+        work = ctx.enter_context(tc.psum_pool(name="work", bufs=5))
+        spool = ctx.enter_context(tc.psum_pool(name="spool", bufs=3))
+
+        ident = const.tile([P, P], F32, name="ident")
+        masks.make_identity(nc, ident[:])
+        ones = const.tile([P, 2], BF16, name="ones")
+        nc.vector.memset(ones[:], 1.0 / NT)
+
+        kseq = [("K", b, s, h) for b in range(B) for s in range(2) for h in range(2)]
+        xseq = [("X", b, s, h) for b in range(B) for h in range(2) for s in range(2)]
+        order = list(kseq[:LEAD])
+        rest = list(kseq[LEAD:])
+        for j, x in enumerate(xseq):
+            order.append(x)
+            if j < len(rest):
+                order.append(rest[j])
+        nstep = len(order)
+
+        srcs = {("K", 0): k, ("K", 1): ki, ("X", 0): xs, ("X", 1): xis}
+        raw = {}
+        qraw = {}
+        qT = {}
+        kT = {}
+        grp = {}
+        cod = {}
+        sca = {}
+        sps = {}
+        mx2 = {}
+        nb = {}
+        ee = {}
+        z2 = {}
+        rz = {}
+        ind = {}
+        ab = {}
+        tmp = {}
+        wv = {}
+        cnt = {"evac": 0, "mm": 0}
+
+        def evac_engine():
+            e = EVAC[cnt["evac"] % len(EVAC)]
+            cnt["evac"] += 1
+            return e
+
+        def copy_out(dst, src):
+            if evac_engine() == "v":
+                nc.vector.tensor_copy(out=dst, in_=src)
+            else:
+                nc.scalar.copy(out=dst, in_=src)
+
+        def load_wv():
+            wr = const.tile([P, 4, 2, DV], BF16, name="wv_raw")
+            nc.sync.dma_start(
+                out=wr[:].rearrange("p s e d -> p s (e d)"),
+                in_=Wv.rearrange("(s p e) d -> p s (e d)", s=4, p=P, e=2),
+            )
+            wv["raw"] = wr
+
+        def prep_wv():
+            wr = wv["raw"]
+            wg = const.tile([P, 2, DV, 2, 2], BF16, name="wv_grp", align_bytes=64)
+            for g in range(2):
+                nc.vector.tensor_copy(
+                    out=wg[:, g],
+                    in_=wr[:, 2 * g : 2 * g + 2].rearrange("p u e d -> p d u e"),
+                )
+            wc = const.tile([P, 2 * DV], U32, name="wv_c", align_bytes=64)
+            ws = const.tile([P, 2 * DV], U8, name="wv_s", align_bytes=64)
+            nc.vector.quantize_mx(
+                out=wc[:].bitcast(FP8X4),
+                scales=ws[:],
+                in_=wg[:].rearrange("p g d u e -> p (g d u e)"),
+            )
+            wv["c"] = wc
+            wv["s"] = ws
+
+        def load(i):
+            kind, b, s, h = order[i]
+            if kind == "K" and s == 0 and h == 0:
+                qr = qp.tile([P, C], BF16, name="qraw", tag="qraw")
+                nc.sync.dma_start(out=qr[:], in_=q[b])
+                qraw[b] = qr
+            if kind == "X" and "raw" not in wv:
+                load_wv()
+            r = rawp.tile([P, 4, C], BF16, name="raw", tag="raw")
+            src = srcs[(kind, s)][b].rearrange("(p t) c -> p t c", t=8)
+            nc.sync.dma_start(out=r[:], in_=src[:, 4 * h : 4 * h + 4, :])
+            raw[i] = r
+
+        def q_transpose(b):
+            w = work.tile([P, 4, P], F32, name="wq", tag="w")
+            qf = qraw[b][:].bitcast(F32)
+            for u in range(4):
+                nc.tensor.transpose(w[:, u, :], qf[:, P * u : P * (u + 1)], ident[:])
+            t = qp.tile([P, 4, 2, P], BF16, name="qT", tag="qT")
+            nc.vector.tensor_copy(
+                out=t[:],
+                in_=w[:].bitcast(BF16).rearrange("p u (n e) -> p u e n", e=2),
+            )
+            qT[b] = t
+
+        def score_mms(job):
+            kind, b, s, h = order[job]
+            acc = spool.tile([P, 512], F32, name="sacc", tag="s")
+            sps[(b, s, h)] = acc
+            kb = kT[job][:].bitcast(BF16).rearrange("p u (n e) -> p u n e", e=2)
+            res = []
+            for u in range(4):
+                for e in range(2):
+                    res.append((acc, qT[b], kb, u, e))
+            return res
+
+        def emit_mm(m):
+            acc, qt, kb, u, e = m
+            nc.tensor.matmul(
+                out=acc[:],
+                lhsT=qt[:, u, e, :],
+                rhs=kb[:, u, :, e],
+                start=(u == 0 and e == 0),
+                stop=(u == 3 and e == 1),
+            )
+
+        def next_mm(mms):
+            if cnt["mm"] < len(mms):
+                emit_mm(mms[cnt["mm"]])
+                cnt["mm"] += 1
+
+        def transposes(i, mms):
+            kind, b, s, h = order[i]
+            rf = raw[i][:].bitcast(F32)
+            if kind == "K":
+                dst = ktp.tile([P, 4, 512], F32, name="kT", tag="kT")
+                kT[i] = dst
+            else:
+                dst = grpp.tile([P, 4 * C], BF16, name="grp", tag="grp", align_bytes=64)
+                grp[i] = dst
+                dstf = dst[:].bitcast(F32).rearrange(
+                    "p (t g n u) -> p t g n u", t=4, g=2, n=P, u=2
+                )
+            for t in range(4):
+                w = work.tile([P, 4, P], F32, name="wt", tag="w")
+                for u in range(4):
+                    if u % 2 == 0:
+                        next_mm(mms)
+                    nc.tensor.transpose(
+                        w[:, u, :], rf[:, t, P * u : P * (u + 1)], ident[:]
+                    )
+                if kind == "K":
+                    copy_out(dst[:, :, P * t : P * (t + 1)], w[:])
+                else:
+                    copy_out(
+                        dstf[:, t], w[:].rearrange("p (g u) n -> p g n u", g=2, u=2)
+                    )
+
+        def quantise(i):
+            c = codp.tile([P, C], U32, name="cod", tag="cod", align_bytes=64)
+            sc = codp.tile([P, C], U8, name="sca", tag="sca", align_bytes=64)
+            nc.vector.quantize_mx(out=c[:].bitcast(FP8X4), scales=sc[:], in_=grp[i][:])
+            cod[i] = c
+            sca[i] = sc
+
+        def rowmax(b, s, h):
+            if h == 0:
+                mx2[(b, s)] = stp.tile([P, 2], F32, name="mx2", tag="mx2")
+            nc.vector.reduce_max(
+                out=mx2[(b, s)][:, h : h + 1], in_=sps[(b, s, h)][:], axis=AX.X
+            )
+
+        def softmax(b, s):
+            m = mx2[(b, s)]
+            nbt = stp.tile([P, 1], F32, name="nb", tag="nb")
+            nc.vector.tensor_scalar(
+                out=nbt[:],
+                in0=m[:, 0:1],
+                scalar1=m[:, 1:2],
+                scalar2=-SCALE,
+                op0=ALU.max,
+                op1=ALU.mult,
+            )
+            e = ep.tile([P, N], F32, name="e%d" % s, tag="e%d" % s)
+            zz = stp.tile([P, 2], F32, name="z2", tag="z2")
+            for h in range(2):
+                nc.scalar.activation(
+                    out=e[:, 512 * h : 512 * (h + 1)],
+                    in_=sps[(b, s, h)][:],
+                    func=ACTF.Exp,
+                    bias=nbt[:, 0:1],
+                    scale=SCALE,
+                    accum_out=zz[:, h : h + 1],
+                )
+            z = stp.tile([P, 1], F32, name="z", tag="z")
+            nc.vector.tensor_tensor(out=z[:], in0=zz[:, 0:1], in1=zz[:, 1:2], op=ALU.add)
+            r = stp.tile([P, 1], F32, name="rz", tag="rz")
+            nc.vector.reciprocal(out=r[:], in_=z[:])
+            ee[(b, s)] = e
+            rz[(b, s)] = r
+
+        def votes(b):
+            e0, e1 = ee[(b, 0)], ee[(b, 1)]
+            nc.vector.tensor_scalar(
+                out=e1[:], in0=e1[:], scalar1=rz[(b, 1)][:, 0:1], scalar2=None, op0=ALU.mult
+            )
+            ge = ep.tile([P, N], BF16, name="ge", tag="ge")
+            le = ep.tile([P, N], BF16, name="le", tag="le")
+            for o, op in ((ge, ALU.is_ge), (le, ALU.is_le)):
+                nc.vector.scalar_tensor_tensor(
+                    out=o[:],
+                    in0=e0[:],
+                    scalar=rz[(b, 0)][:, 0:1],
+                    in1=e1[:],
+                    op0=ALU.mult,
+                    op1=op,
+                )
+            ind[b] = (ge, le)
+
+        def counts(b):
+            w = work.tile([P, 8, 2, 2], F32, name="wc", tag="w")
+            for t in range(8):
+                for j in range(2):
+                    nc.tensor.matmul(
+                        out=w[:, t, j, :],
+                        lhsT=ind[b][j][:, P * t : P * (t + 1)],
+                        rhs=ones[:],
+                        start=True,
+                        stop=True,
+                    )
+            a = abp.tile([P, 8, 2, 2], F32, name="ab", tag="ab")
+            nc.vector.tensor_copy(out=a[:], in_=w[:])
+            ab[b] = a
+
+        def mx_job(i):
+            kind, b, s, h = order[i]
+            if s == 0:
+                dst = outp.tile([P, 4, DV], F32, name="tmp", tag="tmp")
+                tmp[(b, h)] = dst
+            else:
+                dst = outp.tile([P, 4, DV], F32, name="osb", tag="osb")
+            for j in range(2):
+                w = work.tile([P, 2, DV], F32, name="wv", tag="w")
+                for jj in range(2):
+                    t = 2 * j + jj
+                    for g in range(2):
+                        cs = slice((2 * t + g) * P, (2 * t + g + 1) * P)
+                        ws = slice(g * DV, (g + 1) * DV)
+                        nc.tensor.matmul_mx(
+                            out=w[:, jj, :],
+                            lhsT=cod[i][:, cs].bitcast(FP8X4),
+                            lhsT_scale=sca[i][:, cs],
+                            rhs=wv["c"][:, ws].bitcast(FP8X4),
+                            rhs_scale=wv["s"][:, ws],
+                            start=(g == 0),
+                            stop=(g == 1),
+                        )
+                for jj in range(2):
+                    t = 2 * j + jj
+                    gt = 4 * h + t
+                    if s == 0:
+                        nc.scalar.activation(
+                            out=dst[:, t, :],
+                            in_=w[:, jj, :],
+                            func=ACTF.Copy,
+                            scale=ab[b][:, gt, 0, 0:1],
+                        )
+                    else:
+                        nc.vector.scalar_tensor_tensor(
+                            out=dst[:, t, :],
+                            in0=w[:, jj, :],
+                            scalar=ab[b][:, gt, 1, 0:1],
+                            in1=tmp[(b, h)][:, t, :],
+                            op0=ALU.mult,
+                            op1=ALU.add,
+                        )
+            if s == 1:
+                o = out[b].rearrange("(p t) d -> p t d", t=8)
+                nc.gpsimd.dma_start(out=o[:, 4 * h : 4 * h + 4, :], in_=dst[:])
+
+        sq = []
+        xq = []
+        post = {}
+
+        def later(step, item):
+            post[step] = post.get(step, []) + [item]
+
+        for i in range(AHEAD):
+            load(i)
+        i = 0
+        while i < nstep or sq or xq or [st for st in post if st >= i]:
+            if i + AHEAD < nstep:
+                load(i + AHEAD)
+            todo = post.get(i, [])
+            for item in todo:
+                if item[0] == "rm":
+                    rowmax(item[1], item[2], item[3])
+                    if item[3] == 1:
+                        softmax(item[1], item[2])
+            if i >= 1 and i - 1 < nstep and order[i - 1][0] == "X":
+                if "c" not in wv:
+                    prep_wv()
+                quantise(i - 1)
+                xq.append(i - 1)
+            mms = []
+            cnt["mm"] = 0
+            if sq and sq[0] <= i - 2:
+                job = sq[0]
+                sq = sq[1:]
+                mms = score_mms(job)
+                kind, b, s, h = order[job]
+                later(i + 1, ("rm", b, s, h))
+                if s == 1 and h == 1:
+                    later(i + 2, ("votes", b))
+                    later(i + 3, ("counts", b))
+            if i < nstep:
+                kind, b, s, h = order[i]
+                if kind == "K" and s == 0 and h == 0:
+                    q_transpose(b)
+                transposes(i, mms)
+                if kind == "K":
+                    sq.append(i)
+            while cnt["mm"] < len(mms):
+                next_mm(mms)
+            for item in todo:
+                if item[0] == "votes":
+                    votes(item[1])
+            for item in todo:
+                if item[0] == "counts":
+                    counts(item[1])
+            if xq and xq[0] <= i - 2:
+                mx_job(xq[0])
+                xq = xq[1:]
+            i += 1

@@ -1,9 +1,7 @@
 from contextlib import ExitStack
 
-import concourse.bass as bass
 import concourse.masks as masks
 import concourse.mybir as mybir
-import concourse.tile as tile
 
 F32 = mybir.dt.float32
 BF16 = mybir.dt.bfloat16
@@ -20,10 +18,10 @@ FLOPS = 2 * 2 * B * NT * N * C + 2 * 2 * B * N * C * DV
 SCALE = 1.0 / 32.0
 
 MANUAL = True
-LEAD = 6
+WEAVE = True
 NB = 8
 AHEAD = 7
-EVAC = ("s", "s", "v", "s")
+FIX = 60
 
 
 def tile_crossattention_for_fusion_temporal_pa_t_kernel(tc, q, k, ki, xs, xis, Wv, out):
@@ -39,25 +37,19 @@ def tile_crossattention_for_fusion_temporal_pa_t_kernel(tc, q, k, ki, xs, xis, W
         codp = ctx.enter_context(tc.tile_pool(name="codp", bufs=4))
         ep = ctx.enter_context(tc.tile_pool(name="ep", bufs=2))
         stp = ctx.enter_context(tc.tile_pool(name="stp", bufs=4))
-        abp = ctx.enter_context(tc.tile_pool(name="abp", bufs=3))
+        abp = ctx.enter_context(tc.tile_pool(name="abp", bufs=4))
         outp = ctx.enter_context(tc.tile_pool(name="outp", bufs=3))
-        work = ctx.enter_context(tc.psum_pool(name="work", bufs=5))
-        spool = ctx.enter_context(tc.psum_pool(name="spool", bufs=3))
+        psum = ctx.enter_context(tc.psum_pool(name="psum", bufs=1))
 
         ident = const.tile([P, P], F32, name="ident")
         masks.make_identity(nc, ident[:])
         ones = const.tile([P, 2], BF16, name="ones")
         nc.vector.memset(ones[:], 1.0 / NT)
 
-        kseq = [("K", b, s, h) for b in range(B) for s in range(2) for h in range(2)]
-        xseq = [("X", b, s, h) for b in range(B) for h in range(2) for s in range(2)]
-        order = list(kseq[:LEAD])
-        rest = list(kseq[LEAD:])
-        for j, x in enumerate(xseq):
-            order.append(x)
-            if j < len(rest):
-                order.append(rest[j])
+        order = [("K", b, s, h) for b in range(B) for s in range(2) for h in range(2)]
+        order += [("X", b, s, h) for b in range(B) for h in range(2) for s in range(2)]
         nstep = len(order)
+        NK = 16
 
         srcs = {("K", 0): k, ("K", 1): ki, ("X", 0): xs, ("X", 1): xis}
         raw = {}
@@ -69,25 +61,36 @@ def tile_crossattention_for_fusion_temporal_pa_t_kernel(tc, q, k, ki, xs, xis, W
         sca = {}
         sps = {}
         mx2 = {}
-        nb = {}
+        nbs = {}
         ee = {}
         z2 = {}
         rz = {}
         ind = {}
         ab = {}
         tmp = {}
+        osb = {}
         wv = {}
-        cnt = {"evac": 0, "mm": 0}
+        st = {"v": 0, "s": 0, "mm": 0, "wb": 0, "sb": 0, "nwork": 5}
 
-        def evac_engine():
-            e = EVAC[cnt["evac"] % len(EVAC)]
-            cnt["evac"] += 1
-            return e
+        def work_bank(shape, name):
+            n = st["wb"] % st["nwork"]
+            st["wb"] += 1
+            return psum.tile(shape, F32, name=name, tag="bank%d" % n)
+
+        def score_bank():
+            n = 5 + st["sb"] % 3
+            st["sb"] += 1
+            return psum.tile([P, 512], F32, name="sacc", tag="bank%d" % n)
+
+        def charge(eng, cols):
+            st[eng] += cols + FIX
 
         def copy_out(dst, src):
-            if evac_engine() == "v":
+            if st["v"] <= st["s"]:
+                charge("v", 512)
                 nc.vector.tensor_copy(out=dst, in_=src)
             else:
+                charge("s", 512)
                 nc.scalar.copy(out=dst, in_=src)
 
         def load_wv():
@@ -115,22 +118,32 @@ def tile_crossattention_for_fusion_temporal_pa_t_kernel(tc, q, k, ki, xs, xis, W
             )
             wv["c"] = wc
             wv["s"] = ws
+            charge("v", 1500)
+
+        def load_q(b):
+            qr = qp.tile([P, C], BF16, name="qraw", tag="qraw", bufs=4)
+            nc.sync.dma_start(out=qr[:], in_=q[b])
+            qraw[b] = qr
 
         def load(i):
             kind, b, s, h = order[i]
-            if kind == "K" and s == 0 and h == 0:
-                qr = qp.tile([P, C], BF16, name="qraw", tag="qraw")
-                nc.sync.dma_start(out=qr[:], in_=q[b])
-                qraw[b] = qr
-            if kind == "X" and "raw" not in wv:
-                load_wv()
+            if i == 0:
+                load_q(0)
             r = rawp.tile([P, 4, C], BF16, name="raw", tag="raw")
             src = srcs[(kind, s)][b].rearrange("(p t) c -> p t c", t=8)
-            nc.sync.dma_start(out=r[:], in_=src[:, 4 * h : 4 * h + 4, :])
+            if i == 0:
+                for t in range(4):
+                    nc.sync.dma_start(out=r[:, t, :], in_=src[:, t, :])
+            else:
+                nc.sync.dma_start(out=r[:], in_=src[:, 4 * h : 4 * h + 4, :])
             raw[i] = r
+            if kind == "K" and s == 0 and h == 0 and b + 1 < B:
+                load_q(b + 1)
+            if i == 9:
+                load_wv()
 
         def q_transpose(b):
-            w = work.tile([P, 4, P], F32, name="wq", tag="w")
+            w = work_bank([P, 4, P], "wq")
             qf = qraw[b][:].bitcast(F32)
             for u in range(4):
                 nc.tensor.transpose(w[:, u, :], qf[:, P * u : P * (u + 1)], ident[:])
@@ -139,35 +152,29 @@ def tile_crossattention_for_fusion_temporal_pa_t_kernel(tc, q, k, ki, xs, xis, W
                 out=t[:],
                 in_=w[:].bitcast(BF16).rearrange("p u (n e) -> p u e n", e=2),
             )
+            charge("v", 1024)
             qT[b] = t
 
         def score_mms(job):
             kind, b, s, h = order[job]
-            acc = spool.tile([P, 512], F32, name="sacc", tag="s")
+            acc = score_bank()
             sps[(b, s, h)] = acc
             kb = kT[job][:].bitcast(BF16).rearrange("p u (n e) -> p u n e", e=2)
-            res = []
-            for u in range(4):
-                for e in range(2):
-                    res.append((acc, qT[b], kb, u, e))
-            return res
-
-        def emit_mm(m):
-            acc, qt, kb, u, e = m
-            nc.tensor.matmul(
-                out=acc[:],
-                lhsT=qt[:, u, e, :],
-                rhs=kb[:, u, :, e],
-                start=(u == 0 and e == 0),
-                stop=(u == 3 and e == 1),
-            )
+            return [(acc, qT[b], kb, u, e) for u in range(4) for e in range(2)]
 
         def next_mm(mms):
-            if cnt["mm"] < len(mms):
-                emit_mm(mms[cnt["mm"]])
-                cnt["mm"] += 1
+            if st["mm"] < len(mms):
+                acc, qt, kb, u, e = mms[st["mm"]]
+                st["mm"] += 1
+                nc.tensor.matmul(
+                    out=acc[:],
+                    lhsT=qt[:, u, e, :],
+                    rhs=kb[:, u, :, e],
+                    start=(u == 0 and e == 0),
+                    stop=(u == 3 and e == 1),
+                )
 
-        def transposes(i, mms):
+        def transposes(i, mms, hook, last):
             kind, b, s, h = order[i]
             rf = raw[i][:].bitcast(F32)
             if kind == "K":
@@ -180,26 +187,37 @@ def tile_crossattention_for_fusion_temporal_pa_t_kernel(tc, q, k, ki, xs, xis, W
                     "p (t g n u) -> p t g n u", t=4, g=2, n=P, u=2
                 )
             for t in range(4):
-                w = work.tile([P, 4, P], F32, name="wt", tag="w")
+                w = work_bank([P, 4, P], "wt")
                 for u in range(4):
-                    if u % 2 == 0:
+                    if WEAVE and u % 2 == 0:
                         next_mm(mms)
                     nc.tensor.transpose(
                         w[:, u, :], rf[:, t, P * u : P * (u + 1)], ident[:]
                     )
+                if hook and t == 0:
+                    st["s"] = min(st["s"], st["v"] - 1)
                 if kind == "K":
                     copy_out(dst[:, :, P * t : P * (t + 1)], w[:])
                 else:
                     copy_out(
                         dstf[:, t], w[:].rearrange("p (g u) n -> p g n u", g=2, u=2)
                     )
+                if hook and t == 0:
+                    exps(hook[0], hook[1])
+                if last and t == 1:
+                    quantise(i, 0, 2)
 
-        def quantise(i):
-            c = codp.tile([P, C], U32, name="cod", tag="cod", align_bytes=64)
-            sc = codp.tile([P, C], U8, name="sca", tag="sca", align_bytes=64)
-            nc.vector.quantize_mx(out=c[:].bitcast(FP8X4), scales=sc[:], in_=grp[i][:])
-            cod[i] = c
-            sca[i] = sc
+        def quantise(i, part, parts):
+            if part == 0:
+                cod[i] = codp.tile([P, C], U32, name="cod", tag="cod", align_bytes=64)
+                sca[i] = codp.tile([P, C], U8, name="sca", tag="sca", align_bytes=64)
+            w = C // parts
+            cs = slice(part * w, (part + 1) * w)
+            nc.vector.quantize_mx(
+                out=cod[i][:, cs].bitcast(FP8X4),
+                scales=sca[i][:, cs],
+                in_=grp[i][:, 4 * part * w : 4 * (part + 1) * w],
+            )
 
         def rowmax(b, s, h):
             if h == 0:
@@ -208,9 +226,10 @@ def tile_crossattention_for_fusion_temporal_pa_t_kernel(tc, q, k, ki, xs, xis, W
                 out=mx2[(b, s)][:, h : h + 1], in_=sps[(b, s, h)][:], axis=AX.X
             )
 
-        def softmax(b, s):
+        def negmax(b, s):
             m = mx2[(b, s)]
             nbt = stp.tile([P, 1], F32, name="nb", tag="nb")
+            nbs[(b, s)] = nbt
             nc.vector.tensor_scalar(
                 out=nbt[:],
                 in0=m[:, 0:1],
@@ -219,6 +238,9 @@ def tile_crossattention_for_fusion_temporal_pa_t_kernel(tc, q, k, ki, xs, xis, W
                 op0=ALU.max,
                 op1=ALU.mult,
             )
+
+        def exps(b, s):
+            nbt = nbs[(b, s)]
             e = ep.tile([P, N], F32, name="e%d" % s, tag="e%d" % s)
             zz = stp.tile([P, 2], F32, name="z2", tag="z2")
             for h in range(2):
@@ -230,38 +252,44 @@ def tile_crossattention_for_fusion_temporal_pa_t_kernel(tc, q, k, ki, xs, xis, W
                     scale=SCALE,
                     accum_out=zz[:, h : h + 1],
                 )
-            z = stp.tile([P, 1], F32, name="z", tag="z")
-            nc.vector.tensor_tensor(out=z[:], in0=zz[:, 0:1], in1=zz[:, 1:2], op=ALU.add)
-            r = stp.tile([P, 1], F32, name="rz", tag="rz")
-            nc.vector.reciprocal(out=r[:], in_=z[:])
             ee[(b, s)] = e
-            rz[(b, s)] = r
+            z2[(b, s)] = zz
 
-        def votes(b):
-            e0, e1 = ee[(b, 0)], ee[(b, 1)]
+        def compare(b, j):
+            o = ep.tile([P, N], BF16, name="ind%d" % j, tag="ind%d" % j)
+            nc.vector.scalar_tensor_tensor(
+                out=o[:],
+                in0=ee[(b, 0)][:],
+                scalar=rz[(b, 0)][:, 0:1],
+                in1=ee[(b, 1)][:],
+                op0=ALU.mult,
+                op1=(ALU.is_ge if j == 0 else ALU.is_le),
+            )
+            ind[(b, j)] = o
+
+        def votes_a(b):
+            for s in range(2):
+                zz = z2[(b, s)]
+                z = stp.tile([P, 1], F32, name="z", tag="z")
+                nc.vector.tensor_tensor(
+                    out=z[:], in0=zz[:, 0:1], in1=zz[:, 1:2], op=ALU.add
+                )
+                r = stp.tile([P, 1], F32, name="rz", tag="rz")
+                nc.vector.reciprocal(out=r[:], in_=z[:])
+                rz[(b, s)] = r
+            e1 = ee[(b, 1)]
             nc.vector.tensor_scalar(
                 out=e1[:], in0=e1[:], scalar1=rz[(b, 1)][:, 0:1], scalar2=None, op0=ALU.mult
             )
-            ge = ep.tile([P, N], BF16, name="ge", tag="ge")
-            le = ep.tile([P, N], BF16, name="le", tag="le")
-            for o, op in ((ge, ALU.is_ge), (le, ALU.is_le)):
-                nc.vector.scalar_tensor_tensor(
-                    out=o[:],
-                    in0=e0[:],
-                    scalar=rz[(b, 0)][:, 0:1],
-                    in1=e1[:],
-                    op0=ALU.mult,
-                    op1=op,
-                )
-            ind[b] = (ge, le)
+            compare(b, 0)
 
         def counts(b):
-            w = work.tile([P, 8, 2, 2], F32, name="wc", tag="w")
+            w = work_bank([P, 8, 2, 2], "wc")
             for t in range(8):
                 for j in range(2):
                     nc.tensor.matmul(
                         out=w[:, t, j, :],
-                        lhsT=ind[b][j][:, P * t : P * (t + 1)],
+                        lhsT=ind[(b, j)][:, P * t : P * (t + 1)],
                         rhs=ones[:],
                         start=True,
                         stop=True,
@@ -270,15 +298,17 @@ def tile_crossattention_for_fusion_temporal_pa_t_kernel(tc, q, k, ki, xs, xis, W
             nc.vector.tensor_copy(out=a[:], in_=w[:])
             ab[b] = a
 
-        def mx_job(i):
+        def mx_bank(i, j, fine):
             kind, b, s, h = order[i]
-            if s == 0:
-                dst = outp.tile([P, 4, DV], F32, name="tmp", tag="tmp")
-                tmp[(b, h)] = dst
-            else:
-                dst = outp.tile([P, 4, DV], F32, name="osb", tag="osb")
-            for j in range(2):
-                w = work.tile([P, 2, DV], F32, name="wv", tag="w")
+            if j == 0:
+                if s == 0:
+                    tmp[(b, h)] = outp.tile([P, 4, DV], F32, name="tmp", tag="tmp")
+                else:
+                    osb[(b, h)] = outp.tile([P, 4, DV], F32, name="osb", tag="osb")
+            dst = tmp[(b, h)] if s == 0 else osb[(b, h)]
+            o = out[b].rearrange("(p t) d -> p t d", t=8)
+            if True:
+                w = work_bank([P, 2, DV], "wv")
                 for jj in range(2):
                     t = 2 * j + jj
                     for g in range(2):
@@ -312,61 +342,78 @@ def tile_crossattention_for_fusion_temporal_pa_t_kernel(tc, q, k, ki, xs, xis, W
                             op0=ALU.mult,
                             op1=ALU.add,
                         )
-            if s == 1:
-                o = out[b].rearrange("(p t) d -> p t d", t=8)
-                nc.gpsimd.dma_start(out=o[:, 4 * h : 4 * h + 4, :], in_=dst[:])
+                        if fine:
+                            nc.sync.dma_start(out=o[:, gt, :], in_=dst[:, t, :])
+            if s == 1 and j == 1 and not fine:
+                nc.sync.dma_start(out=o[:, 4 * h : 4 * h + 4, :], in_=dst[:])
+            if s == 1 and j == 0 and i == nstep - 1:
+                nc.sync.dma_start(out=o[:, 4 * h : 4 * h + 2, :], in_=dst[:, 0:2, :])
 
-        sq = []
-        xq = []
-        post = {}
-
-        def later(step, item):
-            post[step] = post.get(step, []) + [item]
+        def mx_job(i):
+            mx_bank(i, 0, False)
+            mx_bank(i, 1, False)
 
         for i in range(AHEAD):
             load(i)
-        i = 0
-        while i < nstep or sq or xq or [st for st in post if st >= i]:
+        q_transpose(0)
+        for i in range(nstep):
             if i + AHEAD < nstep:
                 load(i + AHEAD)
-            todo = post.get(i, [])
-            for item in todo:
-                if item[0] == "rm":
-                    rowmax(item[1], item[2], item[3])
-                    if item[3] == 1:
-                        softmax(item[1], item[2])
-            if i >= 1 and i - 1 < nstep and order[i - 1][0] == "X":
-                if "c" not in wv:
-                    prep_wv()
-                quantise(i - 1)
-                xq.append(i - 1)
+            if i == 19:
+                st["nwork"] = 8
+                st["wb"] = 0
+            jq = i - 1
+            jr = i - 3
+            jm = i - 2
+            if NK <= jq < nstep:
+                charge("v", 1024)
+            if 0 <= jr < NK:
+                charge("v", 512)
+                if jr % 2 == 1:
+                    charge("v", 0)
+                    charge("s", 2 * 512 + 2 * FIX)
+            if 0 <= i - 7 < NK and (i - 7) % 4 == 0:
+                charge("v", 512 + 1024 + 6 * FIX)
+            if 0 <= i - 9 < NK and (i - 9) % 4 == 0:
+                charge("v", 1024)
+            if NK <= jm < nstep:
+                charge("s" if order[jm][2] == 0 else "v", 4 * (DV + FIX))
+
+            hook = None
+            if 0 <= jr < NK:
+                kind, b, s, h = order[jr]
+                rowmax(b, s, h)
+                if h == 1:
+                    negmax(b, s)
+                    hook = (b, s)
+            if i == 12:
+                prep_wv()
+            if NK <= jq < nstep:
+                quantise(jq, 0, 1)
+            if 0 <= i - 7 < NK and (i - 7) % 4 == 0:
+                votes_a((i - 7) // 4)
+            if 0 <= i - 9 < NK and (i - 9) % 4 == 0:
+                compare((i - 9) // 4, 1)
             mms = []
-            cnt["mm"] = 0
-            if sq and sq[0] <= i - 2:
-                job = sq[0]
-                sq = sq[1:]
-                mms = score_mms(job)
-                kind, b, s, h = order[job]
-                later(i + 1, ("rm", b, s, h))
-                if s == 1 and h == 1:
-                    later(i + 2, ("votes", b))
-                    later(i + 3, ("counts", b))
+            st["mm"] = 0
+            if 0 <= i - 2 < NK:
+                mms = score_mms(i - 2)
+            if not WEAVE:
+                while st["mm"] < len(mms):
+                    next_mm(mms)
             if i < nstep:
-                kind, b, s, h = order[i]
-                if kind == "K" and s == 0 and h == 0:
-                    q_transpose(b)
-                transposes(i, mms)
-                if kind == "K":
-                    sq.append(i)
-            while cnt["mm"] < len(mms):
+                transposes(i, mms, hook, i == nstep - 1)
+            while st["mm"] < len(mms):
                 next_mm(mms)
-            for item in todo:
-                if item[0] == "votes":
-                    votes(item[1])
-            for item in todo:
-                if item[0] == "counts":
-                    counts(item[1])
-            if xq and xq[0] <= i - 2:
-                mx_job(xq[0])
-                xq = xq[1:]
-            i += 1
+            if i < NK and i % 4 == 1 and i // 4 + 1 < B:
+                q_transpose(i // 4 + 1)
+            if 0 <= i - 10 < NK and (i - 10) % 4 == 0:
+                counts((i - 10) // 4)
+            if NK <= jm < nstep and i < nstep - 1:
+                mx_job(jm)
+        mx_bank(nstep - 3, 0, False)
+        quantise(nstep - 1, 1, 2)
+        mx_bank(nstep - 3, 1, False)
+        mx_job(nstep - 2)
+        mx_bank(nstep - 1, 0, False)
+        mx_bank(nstep - 1, 1, True)

@@ -45,6 +45,10 @@ def tile_crossattention_for_fusion_temporal_pa_t_kernel(tc, q, k, ki, xs, xis, W
         masks.make_identity(nc, ident[:])
         ones = const.tile([P, 2], BF16, name="ones")
         nc.vector.memset(ones[:], 1.0 / NT)
+        warm0 = const.tile([P, 1], F32, name="warm0")
+        warm1 = const.tile([P, 1], F32, name="warm1")
+        nc.vector.memset(warm0[:], 0.0)
+        nc.scalar.activation(out=warm1[:], in_=warm0[:], func=ACTF.Exp)
 
         order = [("K", b, s, h) for b in range(B) for s in range(2) for h in range(2)]
         order += [("X", b, s, h) for b in range(B) for h in range(2) for s in range(2)]
@@ -148,11 +152,11 @@ def tile_crossattention_for_fusion_temporal_pa_t_kernel(tc, q, k, ki, xs, xis, W
             for u in range(4):
                 nc.tensor.transpose(w[:, u, :], qf[:, P * u : P * (u + 1)], ident[:])
             t = qp.tile([P, 4, 2, P], BF16, name="qT", tag="qT")
-            nc.vector.tensor_copy(
+            nc.scalar.copy(
                 out=t[:],
                 in_=w[:].bitcast(BF16).rearrange("p u (n e) -> p u e n", e=2),
             )
-            charge("v", 1024)
+            charge("s", 1024)
             qT[b] = t
 
         def score_mms(job):
@@ -194,16 +198,12 @@ def tile_crossattention_for_fusion_temporal_pa_t_kernel(tc, q, k, ki, xs, xis, W
                     nc.tensor.transpose(
                         w[:, u, :], rf[:, t, P * u : P * (u + 1)], ident[:]
                     )
-                if hook and t == 0:
-                    st["s"] = min(st["s"], st["v"] - 1)
                 if kind == "K":
                     copy_out(dst[:, :, P * t : P * (t + 1)], w[:])
                 else:
                     copy_out(
                         dstf[:, t], w[:].rearrange("p (g u) n -> p g n u", g=2, u=2)
                     )
-                if hook and t == 0:
-                    exps(hook[0], hook[1])
                 if last and t == 1:
                     quantise(i, 0, 2)
 
@@ -222,8 +222,15 @@ def tile_crossattention_for_fusion_temporal_pa_t_kernel(tc, q, k, ki, xs, xis, W
         def rowmax(b, s, h):
             if h == 0:
                 mx2[(b, s)] = stp.tile([P, 2], F32, name="mx2", tag="mx2")
-            nc.vector.reduce_max(
-                out=mx2[(b, s)][:, h : h + 1], in_=sps[(b, s, h)][:], axis=AX.X
+                ee[(b, s)] = ep.tile([P, N], F32, name="e%d" % s, tag="e%d" % s)
+            nc.vector.tensor_scalar(
+                out=ee[(b, s)][:, 512 * h : 512 * (h + 1)],
+                in0=sps[(b, s, h)][:],
+                scalar1=SCALE,
+                scalar2=None,
+                op0=ALU.mult,
+                op1=ALU.max,
+                accum_out=mx2[(b, s)][:, h : h + 1],
             )
 
         def negmax(b, s):
@@ -234,25 +241,23 @@ def tile_crossattention_for_fusion_temporal_pa_t_kernel(tc, q, k, ki, xs, xis, W
                 out=nbt[:],
                 in0=m[:, 0:1],
                 scalar1=m[:, 1:2],
-                scalar2=-SCALE,
+                scalar2=-1.0,
                 op0=ALU.max,
                 op1=ALU.mult,
             )
 
         def exps(b, s):
             nbt = nbs[(b, s)]
-            e = ep.tile([P, N], F32, name="e%d" % s, tag="e%d" % s)
-            zz = stp.tile([P, 2], F32, name="z2", tag="z2")
-            for h in range(2):
-                nc.scalar.activation(
-                    out=e[:, 512 * h : 512 * (h + 1)],
-                    in_=sps[(b, s, h)][:],
-                    func=ACTF.Exp,
-                    bias=nbt[:, 0:1],
-                    scale=SCALE,
-                    accum_out=zz[:, h : h + 1],
-                )
-            ee[(b, s)] = e
+            e = ee[(b, s)]
+            zz = stp.tile([P, 1], F32, name="z", tag="z")
+            nc.scalar.activation(
+                out=e[:],
+                in_=e[:],
+                func=ACTF.Exp,
+                bias=nbt[:, 0:1],
+                scale=1.0,
+                accum_out=zz[:, 0:1],
+            )
             z2[(b, s)] = zz
 
         def compare(b, j):
@@ -269,13 +274,8 @@ def tile_crossattention_for_fusion_temporal_pa_t_kernel(tc, q, k, ki, xs, xis, W
 
         def votes_a(b):
             for s in range(2):
-                zz = z2[(b, s)]
-                z = stp.tile([P, 1], F32, name="z", tag="z")
-                nc.vector.tensor_tensor(
-                    out=z[:], in0=zz[:, 0:1], in1=zz[:, 1:2], op=ALU.add
-                )
                 r = stp.tile([P, 1], F32, name="rz", tag="rz")
-                nc.vector.reciprocal(out=r[:], in_=z[:])
+                nc.vector.reciprocal(out=r[:], in_=z2[(b, s)][:])
                 rz[(b, s)] = r
             e1 = ee[(b, 1)]
             nc.vector.tensor_scalar(
@@ -371,10 +371,11 @@ def tile_crossattention_for_fusion_temporal_pa_t_kernel(tc, q, k, ki, xs, xis, W
                 charge("v", 512)
                 if jr % 2 == 1:
                     charge("v", 0)
-                    charge("s", 2 * 512 + 2 * FIX)
-            if 0 <= i - 7 < NK and (i - 7) % 4 == 0:
-                charge("v", 512 + 1024 + 6 * FIX)
-            if 0 <= i - 9 < NK and (i - 9) % 4 == 0:
+            if 0 <= jr - 1 < NK and (jr - 1) % 2 == 1:
+                charge("s", 1024 + 2 * FIX)
+            if 0 <= i - 8 < NK and (i - 8) % 4 == 0:
+                charge("v", 512 + 1024 + 4 * FIX)
+            if 0 <= i - 10 < NK and (i - 10) % 4 == 0:
                 charge("v", 1024)
             if NK <= jm < nstep:
                 charge("s" if order[jm][2] == 0 else "v", 4 * (DV + FIX))
@@ -385,15 +386,16 @@ def tile_crossattention_for_fusion_temporal_pa_t_kernel(tc, q, k, ki, xs, xis, W
                 rowmax(b, s, h)
                 if h == 1:
                     negmax(b, s)
-                    hook = (b, s)
+            if 0 <= jr - 1 < NK and (jr - 1) % 2 == 1:
+                exps(order[jr - 1][1], order[jr - 1][2])
             if i == 12:
                 prep_wv()
             if NK <= jq < nstep:
                 quantise(jq, 0, 1)
-            if 0 <= i - 7 < NK and (i - 7) % 4 == 0:
-                votes_a((i - 7) // 4)
-            if 0 <= i - 9 < NK and (i - 9) % 4 == 0:
-                compare((i - 9) // 4, 1)
+            if 0 <= i - 8 < NK and (i - 8) % 4 == 0:
+                votes_a((i - 8) // 4)
+            if 0 <= i - 10 < NK and (i - 10) % 4 == 0:
+                compare((i - 10) // 4, 1)
             mms = []
             st["mm"] = 0
             if 0 <= i - 2 < NK:
@@ -407,8 +409,8 @@ def tile_crossattention_for_fusion_temporal_pa_t_kernel(tc, q, k, ki, xs, xis, W
                 next_mm(mms)
             if i < NK and i % 4 == 1 and i // 4 + 1 < B:
                 q_transpose(i // 4 + 1)
-            if 0 <= i - 10 < NK and (i - 10) % 4 == 0:
-                counts((i - 10) // 4)
+            if 0 <= i - 11 < NK and (i - 11) % 4 == 0:
+                counts((i - 11) // 4)
             if NK <= jm < nstep and i < nstep - 1:
                 mx_job(jm)
         mx_bank(nstep - 3, 0, False)

@@ -43,6 +43,8 @@ def tile_crossattention_for_fusion_temporal_pa_t_kernel(tc, q, k, ki, xs, xis, W
 
         ident = const.tile([P, P], F32, name="ident")
         masks.make_identity(nc, ident[:])
+        identb = const.tile([P, P], BF16, name="identb")
+        masks.make_identity(nc, identb[:])
         ones = const.tile([P, 2], BF16, name="ones")
         nc.vector.memset(ones[:], 1.0 / NT)
         warm0 = const.tile([P, 1], F32, name="warm0")
@@ -76,10 +78,10 @@ def tile_crossattention_for_fusion_temporal_pa_t_kernel(tc, q, k, ki, xs, xis, W
         wv = {}
         st = {"v": 0, "s": 0, "mm": 0, "wb": 0, "sb": 0, "nwork": 5}
 
-        def work_bank(shape, name):
+        def work_bank(shape, name, dtype=F32):
             n = st["wb"] % st["nwork"]
             st["wb"] += 1
-            return psum.tile(shape, F32, name=name, tag="bank%d" % n)
+            return psum.tile(shape, dtype, name=name, tag="bank%d" % n)
 
         def score_bank():
             n = 5 + st["sb"] % 3
@@ -147,42 +149,38 @@ def tile_crossattention_for_fusion_temporal_pa_t_kernel(tc, q, k, ki, xs, xis, W
                 load_wv()
 
         def q_transpose(b):
-            w = work_bank([P, 4, P], "wq")
-            qf = qraw[b][:].bitcast(F32)
-            for u in range(4):
-                nc.tensor.transpose(w[:, u, :], qf[:, P * u : P * (u + 1)], ident[:])
-            t = qp.tile([P, 4, 2, P], BF16, name="qT", tag="qT")
-            nc.scalar.copy(
-                out=t[:],
-                in_=w[:].bitcast(BF16).rearrange("p u (n e) -> p u e n", e=2),
-            )
-            charge("s", 1024)
+            w = work_bank([P, 8, P], "wq", BF16)
+            for j in range(8):
+                nc.tensor.transpose(
+                    w[:, j, :], qraw[b][:, P * j : P * (j + 1)], identb[:]
+                )
+            t = qp.tile([P, 8, P], BF16, name="qT", tag="qT")
+            copy_out(t[:], w[:])
             qT[b] = t
 
         def score_mms(job):
             kind, b, s, h = order[job]
             acc = score_bank()
             sps[(b, s, h)] = acc
-            kb = kT[job][:].bitcast(BF16).rearrange("p u (n e) -> p u n e", e=2)
-            return [(acc, qT[b], kb, u, e) for u in range(4) for e in range(2)]
+            return [(acc, qT[b], kT[job], j) for j in range(8)]
 
         def next_mm(mms):
             if st["mm"] < len(mms):
-                acc, qt, kb, u, e = mms[st["mm"]]
+                acc, qt, kt, j = mms[st["mm"]]
                 st["mm"] += 1
                 nc.tensor.matmul(
                     out=acc[:],
-                    lhsT=qt[:, u, e, :],
-                    rhs=kb[:, u, :, e],
-                    start=(u == 0 and e == 0),
-                    stop=(u == 3 and e == 1),
+                    lhsT=qt[:, j, :],
+                    rhs=kt[:, j, :],
+                    start=(j == 0),
+                    stop=(j == 7),
                 )
 
         def transposes(i, mms, hook, last):
             kind, b, s, h = order[i]
             rf = raw[i][:].bitcast(F32)
             if kind == "K":
-                dst = ktp.tile([P, 4, 512], F32, name="kT", tag="kT")
+                dst = ktp.tile([P, 8, 512], BF16, name="kT", tag="kT")
                 kT[i] = dst
             else:
                 dst = grpp.tile([P, 4 * C], BF16, name="grp", tag="grp", align_bytes=64)
@@ -191,19 +189,32 @@ def tile_crossattention_for_fusion_temporal_pa_t_kernel(tc, q, k, ki, xs, xis, W
                     "p (t g n u) -> p t g n u", t=4, g=2, n=P, u=2
                 )
             for t in range(4):
-                w = work_bank([P, 4, P], "wt")
-                for u in range(4):
-                    if WEAVE and u % 2 == 0:
-                        next_mm(mms)
-                    nc.tensor.transpose(
-                        w[:, u, :], rf[:, t, P * u : P * (u + 1)], ident[:]
-                    )
+                if kind == "K":
+                    w = work_bank([P, 8, P], "wt", BF16)
+                    for j in range(8):
+                        if WEAVE and j % 4 == 0:
+                            next_mm(mms)
+                        nc.tensor.transpose(
+                            w[:, j, :], raw[i][:, t, P * j : P * (j + 1)], identb[:]
+                        )
+                else:
+                    w = work_bank([P, 4, P], "wt")
+                    for u in range(4):
+                        if WEAVE and u % 2 == 0:
+                            next_mm(mms)
+                        nc.tensor.transpose(
+                            w[:, u, :], rf[:, t, P * u : P * (u + 1)], ident[:]
+                        )
+                if hook and t == 0:
+                    st["s"] = min(st["s"], st["v"] - 1)
                 if kind == "K":
                     copy_out(dst[:, :, P * t : P * (t + 1)], w[:])
                 else:
                     copy_out(
                         dstf[:, t], w[:].rearrange("p (g u) n -> p g n u", g=2, u=2)
                     )
+                if hook and t == 0:
+                    exps(hook[0], hook[1])
                 if last and t == 1:
                     quantise(i, 0, 2)
 
@@ -222,15 +233,8 @@ def tile_crossattention_for_fusion_temporal_pa_t_kernel(tc, q, k, ki, xs, xis, W
         def rowmax(b, s, h):
             if h == 0:
                 mx2[(b, s)] = stp.tile([P, 2], F32, name="mx2", tag="mx2")
-                ee[(b, s)] = ep.tile([P, N], F32, name="e%d" % s, tag="e%d" % s)
-            nc.vector.tensor_scalar(
-                out=ee[(b, s)][:, 512 * h : 512 * (h + 1)],
-                in0=sps[(b, s, h)][:],
-                scalar1=SCALE,
-                scalar2=None,
-                op0=ALU.mult,
-                op1=ALU.max,
-                accum_out=mx2[(b, s)][:, h : h + 1],
+            nc.vector.reduce_max(
+                out=mx2[(b, s)][:, h : h + 1], in_=sps[(b, s, h)][:], axis=AX.X
             )
 
         def negmax(b, s):
@@ -241,23 +245,25 @@ def tile_crossattention_for_fusion_temporal_pa_t_kernel(tc, q, k, ki, xs, xis, W
                 out=nbt[:],
                 in0=m[:, 0:1],
                 scalar1=m[:, 1:2],
-                scalar2=-1.0,
+                scalar2=-SCALE,
                 op0=ALU.max,
                 op1=ALU.mult,
             )
 
         def exps(b, s):
             nbt = nbs[(b, s)]
-            e = ee[(b, s)]
-            zz = stp.tile([P, 1], F32, name="z", tag="z")
-            nc.scalar.activation(
-                out=e[:],
-                in_=e[:],
-                func=ACTF.Exp,
-                bias=nbt[:, 0:1],
-                scale=1.0,
-                accum_out=zz[:, 0:1],
-            )
+            e = ep.tile([P, N], F32, name="e%d" % s, tag="e%d" % s)
+            zz = stp.tile([P, 2], F32, name="z2", tag="z2")
+            for h in range(2):
+                nc.scalar.activation(
+                    out=e[:, 512 * h : 512 * (h + 1)],
+                    in_=sps[(b, s, h)][:],
+                    func=ACTF.Exp,
+                    bias=nbt[:, 0:1],
+                    scale=SCALE,
+                    accum_out=zz[:, h : h + 1],
+                )
+            ee[(b, s)] = e
             z2[(b, s)] = zz
 
         def compare(b, j):
@@ -274,8 +280,13 @@ def tile_crossattention_for_fusion_temporal_pa_t_kernel(tc, q, k, ki, xs, xis, W
 
         def votes_a(b):
             for s in range(2):
+                zz = z2[(b, s)]
+                z = stp.tile([P, 1], F32, name="z", tag="z")
+                nc.vector.tensor_tensor(
+                    out=z[:], in0=zz[:, 0:1], in1=zz[:, 1:2], op=ALU.add
+                )
                 r = stp.tile([P, 1], F32, name="rz", tag="rz")
-                nc.vector.reciprocal(out=r[:], in_=z2[(b, s)][:])
+                nc.vector.reciprocal(out=r[:], in_=z[:])
                 rz[(b, s)] = r
             e1 = ee[(b, 1)]
             nc.vector.tensor_scalar(
@@ -371,11 +382,10 @@ def tile_crossattention_for_fusion_temporal_pa_t_kernel(tc, q, k, ki, xs, xis, W
                 charge("v", 512)
                 if jr % 2 == 1:
                     charge("v", 0)
-            if 0 <= jr - 1 < NK and (jr - 1) % 2 == 1:
-                charge("s", 1024 + 2 * FIX)
-            if 0 <= i - 8 < NK and (i - 8) % 4 == 0:
-                charge("v", 512 + 1024 + 4 * FIX)
-            if 0 <= i - 10 < NK and (i - 10) % 4 == 0:
+                    charge("s", 2 * 512 + 2 * FIX)
+            if 0 <= i - 7 < NK and (i - 7) % 4 == 0:
+                charge("v", 512 + 1024 + 6 * FIX)
+            if 0 <= i - 9 < NK and (i - 9) % 4 == 0:
                 charge("v", 1024)
             if NK <= jm < nstep:
                 charge("s" if order[jm][2] == 0 else "v", 4 * (DV + FIX))
@@ -386,16 +396,15 @@ def tile_crossattention_for_fusion_temporal_pa_t_kernel(tc, q, k, ki, xs, xis, W
                 rowmax(b, s, h)
                 if h == 1:
                     negmax(b, s)
-            if 0 <= jr - 1 < NK and (jr - 1) % 2 == 1:
-                exps(order[jr - 1][1], order[jr - 1][2])
+                    hook = (b, s)
             if i == 12:
                 prep_wv()
             if NK <= jq < nstep:
                 quantise(jq, 0, 1)
-            if 0 <= i - 8 < NK and (i - 8) % 4 == 0:
-                votes_a((i - 8) // 4)
-            if 0 <= i - 10 < NK and (i - 10) % 4 == 0:
-                compare((i - 10) // 4, 1)
+            if 0 <= i - 7 < NK and (i - 7) % 4 == 0:
+                votes_a((i - 7) // 4)
+            if 0 <= i - 9 < NK and (i - 9) % 4 == 0:
+                compare((i - 9) // 4, 1)
             mms = []
             st["mm"] = 0
             if 0 <= i - 2 < NK:
@@ -409,8 +418,8 @@ def tile_crossattention_for_fusion_temporal_pa_t_kernel(tc, q, k, ki, xs, xis, W
                 next_mm(mms)
             if i < NK and i % 4 == 1 and i // 4 + 1 < B:
                 q_transpose(i // 4 + 1)
-            if 0 <= i - 11 < NK and (i - 11) % 4 == 0:
-                counts((i - 11) // 4)
+            if 0 <= i - 10 < NK and (i - 10) % 4 == 0:
+                counts((i - 10) // 4)
             if NK <= jm < nstep and i < nstep - 1:
                 mx_job(jm)
         mx_bank(nstep - 3, 0, False)

@@ -137,9 +137,9 @@ def tile_crossattention_for_fusion_temporal_pa_t_kernel(tc, q, k, ki, xs, xis, W
                 load_q(0)
             r = rawp.tile([P, 4, C], BF16, name="raw", tag="raw")
             src = srcs[(kind, s)][b].rearrange("(p t) c -> p t c", t=8)
-            if i == 0:
+            if i < 3:
                 for t in range(4):
-                    nc.sync.dma_start(out=r[:, t, :], in_=src[:, t, :])
+                    nc.sync.dma_start(out=r[:, t, :], in_=src[:, 4 * h + t, :])
             else:
                 nc.sync.dma_start(out=r[:], in_=src[:, 4 * h : 4 * h + 4, :])
             raw[i] = r
@@ -155,7 +155,7 @@ def tile_crossattention_for_fusion_temporal_pa_t_kernel(tc, q, k, ki, xs, xis, W
                     w[:, j, :], qraw[b][:, P * j : P * (j + 1)], identb[:]
                 )
             t = qp.tile([P, 8, P], BF16, name="qT", tag="qT")
-            copy_out(t[:], w[:])
+            copy_out(t[:].bitcast(F32), w[:].bitcast(F32))
             qT[b] = t
 
         def score_mms(job):
@@ -208,7 +208,9 @@ def tile_crossattention_for_fusion_temporal_pa_t_kernel(tc, q, k, ki, xs, xis, W
                 if hook and t == 0:
                     st["s"] = min(st["s"], st["v"] - 1)
                 if kind == "K":
-                    copy_out(dst[:, :, P * t : P * (t + 1)], w[:])
+                    copy_out(
+                        dst[:, :, P * t : P * (t + 1)].bitcast(F32), w[:].bitcast(F32)
+                    )
                 else:
                     copy_out(
                         dstf[:, t], w[:].rearrange("p (g u) n -> p g n u", g=2, u=2)

@@ -43,8 +43,6 @@ def tile_crossattention_for_fusion_temporal_pa_t_kernel(tc, q, k, ki, xs, xis, W
 
         ident = const.tile([P, P], F32, name="ident")
         masks.make_identity(nc, ident[:])
-        identb = const.tile([P, P], BF16, name="identb")
-        masks.make_identity(nc, identb[:])
         ones = const.tile([P, 2], BF16, name="ones")
         nc.vector.memset(ones[:], 1.0 / NT)
         warm0 = const.tile([P, 1], F32, name="warm0")
@@ -78,10 +76,10 @@ def tile_crossattention_for_fusion_temporal_pa_t_kernel(tc, q, k, ki, xs, xis, W
         wv = {}
         st = {"v": 0, "s": 0, "mm": 0, "wb": 0, "sb": 0, "nwork": 5}
 
-        def work_bank(shape, name, dtype=F32):
+        def work_bank(shape, name):
             n = st["wb"] % st["nwork"]
             st["wb"] += 1
-            return psum.tile(shape, dtype, name=name, tag="bank%d" % n)
+            return psum.tile(shape, F32, name=name, tag="bank%d" % n)
 
         def score_bank():
             n = 5 + st["sb"] % 3
@@ -137,9 +135,9 @@ def tile_crossattention_for_fusion_temporal_pa_t_kernel(tc, q, k, ki, xs, xis, W
                 load_q(0)
             r = rawp.tile([P, 4, C], BF16, name="raw", tag="raw")
             src = srcs[(kind, s)][b].rearrange("(p t) c -> p t c", t=8)
-            if i < 3:
+            if i == 0:
                 for t in range(4):
-                    nc.sync.dma_start(out=r[:, t, :], in_=src[:, 4 * h + t, :])
+                    nc.sync.dma_start(out=r[:, t, :], in_=src[:, t, :])
             else:
                 nc.sync.dma_start(out=r[:], in_=src[:, 4 * h : 4 * h + 4, :])
             raw[i] = r
@@ -149,38 +147,42 @@ def tile_crossattention_for_fusion_temporal_pa_t_kernel(tc, q, k, ki, xs, xis, W
                 load_wv()
 
         def q_transpose(b):
-            w = work_bank([P, 8, P], "wq", BF16)
-            for j in range(8):
-                nc.tensor.transpose(
-                    w[:, j, :], qraw[b][:, P * j : P * (j + 1)], identb[:]
-                )
-            t = qp.tile([P, 8, P], BF16, name="qT", tag="qT")
-            copy_out(t[:].bitcast(F32), w[:].bitcast(F32))
+            w = work_bank([P, 4, P], "wq")
+            qf = qraw[b][:].bitcast(F32)
+            for u in range(4):
+                nc.tensor.transpose(w[:, u, :], qf[:, P * u : P * (u + 1)], ident[:])
+            t = qp.tile([P, 4, 2, P], BF16, name="qT", tag="qT")
+            nc.vector.tensor_copy(
+                out=t[:],
+                in_=w[:].bitcast(BF16).rearrange("p u (n e) -> p u e n", e=2),
+            )
+            charge("v", 1024)
             qT[b] = t
 
         def score_mms(job):
             kind, b, s, h = order[job]
             acc = score_bank()
             sps[(b, s, h)] = acc
-            return [(acc, qT[b], kT[job], j) for j in range(8)]
+            kb = kT[job][:].bitcast(BF16).rearrange("p u (n e) -> p u n e", e=2)
+            return [(acc, qT[b], kb, u, e) for u in range(4) for e in range(2)]
 
         def next_mm(mms):
             if st["mm"] < len(mms):
-                acc, qt, kt, j = mms[st["mm"]]
+                acc, qt, kb, u, e = mms[st["mm"]]
                 st["mm"] += 1
                 nc.tensor.matmul(
                     out=acc[:],
-                    lhsT=qt[:, j, :],
-                    rhs=kt[:, j, :],
-                    start=(j == 0),
-                    stop=(j == 7),
+                    lhsT=qt[:, u, e, :],
+                    rhs=kb[:, u, :, e],
+                    start=(u == 0 and e == 0),
+                    stop=(u == 3 and e == 1),
                 )
 
         def transposes(i, mms, hook, last):
             kind, b, s, h = order[i]
             rf = raw[i][:].bitcast(F32)
             if kind == "K":
-                dst = ktp.tile([P, 8, 512], BF16, name="kT", tag="kT")
+                dst = ktp.tile([P, 4, 512], F32, name="kT", tag="kT")
                 kT[i] = dst
             else:
                 dst = grpp.tile([P, 4 * C], BF16, name="grp", tag="grp", align_bytes=64)
@@ -189,28 +191,18 @@ def tile_crossattention_for_fusion_temporal_pa_t_kernel(tc, q, k, ki, xs, xis, W
                     "p (t g n u) -> p t g n u", t=4, g=2, n=P, u=2
                 )
             for t in range(4):
-                if kind == "K":
-                    w = work_bank([P, 8, P], "wt", BF16)
-                    for j in range(8):
-                        if WEAVE and j % 4 == 0:
-                            next_mm(mms)
-                        nc.tensor.transpose(
-                            w[:, j, :], raw[i][:, t, P * j : P * (j + 1)], identb[:]
-                        )
-                else:
-                    w = work_bank([P, 4, P], "wt")
-                    for u in range(4):
-                        if WEAVE and u % 2 == 0:
-                            next_mm(mms)
-                        nc.tensor.transpose(
-                            w[:, u, :], rf[:, t, P * u : P * (u + 1)], ident[:]
-                        )
+                w = work_bank([P, 4, P], "wt")
+                for u in range(4):
+                    if WEAVE and u == 0:
+                        next_mm(mms)
+                        next_mm(mms)
+                    nc.tensor.transpose(
+                        w[:, u, :], rf[:, t, P * u : P * (u + 1)], ident[:]
+                    )
                 if hook and t == 0:
                     st["s"] = min(st["s"], st["v"] - 1)
                 if kind == "K":
-                    copy_out(
-                        dst[:, :, P * t : P * (t + 1)].bitcast(F32), w[:].bitcast(F32)
-                    )
+                    copy_out(dst[:, :, P * t : P * (t + 1)], w[:])
                 else:
                     copy_out(
                         dstf[:, t], w[:].rearrange("p (g u) n -> p g n u", g=2, u=2)

@@ -9,416 +9,373 @@ U32 = mybir.dt.uint32
 U8 = mybir.dt.uint8
 FP8X4 = mybir.dt.float8_e4m3fn_x4
 ALU = mybir.AluOpType
-ACTF = mybir.ActivationFunctionType
-AX = mybir.AxisListType
+ACT = mybir.ActivationFunctionType
+AXIS = mybir.AxisListType
 
 B, NT, N, C, DV = 4, 128, 1024, 1024, 256
 P = 128
+HALF = N // 2
+TILES = HALF // P
+WCOLS = C // (2 * P)
 FLOPS = 2 * 2 * B * NT * N * C + 2 * 2 * B * N * C * DV
 SCALE = 1.0 / 32.0
 
-MANUAL = True
-WEAVE = True
-NB = 8
-AHEAD = 7
-FIX = 60
+PER_BATCH = 4
+KEY_STEPS = PER_BATCH * B
+STEPS = 2 * KEY_STEPS
+RAW_BUFS = 8
+AHEAD = RAW_BUFS - 1
+
+SCORE_LAG = 2
+MAX_LAG = 3
+QUANT_LAG = 1
+MX_LAG = 2
+GE_LAG = 4
+LE_LAG = 6
+COUNT_LAG = 7
+
+SCORE_BANKS = 3
+WORK_BANKS = 5
+ALL_BANKS = 8
+LAST_SCORE_STEP = KEY_STEPS - 1 + MAX_LAG
 
 
 def tile_crossattention_for_fusion_temporal_pa_t_kernel(tc, q, k, ki, xs, xis, Wv, out):
     nc = tc.nc
     with ExitStack() as ctx:
-        if MANUAL:
-            ctx.enter_context(tc.manual_schedule())
+        ctx.enter_context(tc.manual_schedule())
         const = ctx.enter_context(tc.tile_pool(name="const", bufs=1))
-        rawp = ctx.enter_context(tc.tile_pool(name="rawp", bufs=NB))
+        rawp = ctx.enter_context(tc.tile_pool(name="rawp", bufs=RAW_BUFS))
         qp = ctx.enter_context(tc.tile_pool(name="qp", bufs=2))
         ktp = ctx.enter_context(tc.tile_pool(name="ktp", bufs=4))
         grpp = ctx.enter_context(tc.tile_pool(name="grpp", bufs=3))
         codp = ctx.enter_context(tc.tile_pool(name="codp", bufs=4))
         ep = ctx.enter_context(tc.tile_pool(name="ep", bufs=2))
         stp = ctx.enter_context(tc.tile_pool(name="stp", bufs=4))
-        abp = ctx.enter_context(tc.tile_pool(name="abp", bufs=4))
+        abp = ctx.enter_context(tc.tile_pool(name="abp", bufs=B))
         outp = ctx.enter_context(tc.tile_pool(name="outp", bufs=3))
         psum = ctx.enter_context(tc.psum_pool(name="psum", bufs=1))
 
         ident = const.tile([P, P], F32, name="ident")
         masks.make_identity(nc, ident[:])
-        ones = const.tile([P, 2], BF16, name="ones")
-        nc.vector.memset(ones[:], 1.0 / NT)
-        warm0 = const.tile([P, 1], F32, name="warm0")
-        warm1 = const.tile([P, 1], F32, name="warm1")
-        nc.vector.memset(warm0[:], 0.0)
-        nc.scalar.activation(out=warm1[:], in_=warm0[:], func=ACTF.Exp)
+        share = const.tile([P, 2], BF16, name="share")
+        nc.vector.memset(share[:], 1.0 / NT)
 
-        order = [("K", b, s, h) for b in range(B) for s in range(2) for h in range(2)]
-        order += [("X", b, s, h) for b in range(B) for h in range(2) for s in range(2)]
-        nstep = len(order)
-        NK = 16
+        halves = [("key", b, stream, h) for b in range(B) for stream in range(2) for h in range(2)]
+        halves += [("val", b, stream, h) for b in range(B) for h in range(2) for stream in range(2)]
+        dram = {("key", 0): k, ("key", 1): ki, ("val", 0): xs, ("val", 1): xis}
 
-        srcs = {("K", 0): k, ("K", 1): ki, ("X", 0): xs, ("X", 1): xis}
-        raw = {}
-        qraw = {}
-        qT = {}
-        kT = {}
-        grp = {}
-        cod = {}
-        sca = {}
-        sps = {}
-        mx2 = {}
-        nbs = {}
-        ee = {}
-        z2 = {}
-        rz = {}
-        ind = {}
-        ab = {}
-        tmp = {}
-        osb = {}
-        wv = {}
-        st = {"v": 0, "s": 0, "mm": 0, "wb": 0, "sb": 0, "nwork": 5}
+        raw, q_raw, q_t, k_t, grouped, codes, scales = {}, {}, {}, {}, {}, {}, {}
+        score, row_max, neg_max, expo, exp_sum, inv_sum, vote, ratio = {}, {}, {}, {}, {}, {}, {}, {}
+        first_mix, mixed, wv = {}, {}, {}
+        turn = {"work": 0, "work_banks": WORK_BANKS, "score": 0}
 
         def work_bank(shape, name):
-            n = st["wb"] % st["nwork"]
-            st["wb"] += 1
-            return psum.tile(shape, F32, name=name, tag="bank%d" % n)
+            bank = turn["work"] % turn["work_banks"]
+            turn["work"] += 1
+            return psum.tile(shape, F32, name=name, tag="bank%d" % bank)
 
         def score_bank():
-            n = 5 + st["sb"] % 3
-            st["sb"] += 1
-            return psum.tile([P, 512], F32, name="sacc", tag="bank%d" % n)
+            bank = WORK_BANKS + turn["score"] % SCORE_BANKS
+            turn["score"] += 1
+            return psum.tile([P, HALF], F32, name="sacc", tag="bank%d" % bank)
 
-        def charge(eng, cols):
-            st[eng] += cols + FIX
+        def batch_due(i, lag):
+            j = i - lag
+            if 0 <= j < KEY_STEPS and j % PER_BATCH == PER_BATCH - 1:
+                return j // PER_BATCH
+            return None
 
-        def copy_out(dst, src):
-            if st["v"] <= st["s"]:
-                charge("v", 512)
+        def second_mix_due(i):
+            j = i - MX_LAG
+            return KEY_STEPS <= j < STEPS and halves[j][2] == 1
+
+        def vector_is_taken(i):
+            return (
+                batch_due(i, GE_LAG) is not None
+                or batch_due(i, LE_LAG) is not None
+                or second_mix_due(i)
+            )
+
+        def copy_out(i, t, dst, src):
+            if t % 2 == 1 and not vector_is_taken(i):
                 nc.vector.tensor_copy(out=dst, in_=src)
             else:
-                charge("s", 512)
                 nc.scalar.copy(out=dst, in_=src)
 
-        def load_wv():
-            wr = const.tile([P, 4, 2, DV], BF16, name="wv_raw")
-            nc.sync.dma_start(
-                out=wr[:].rearrange("p s e d -> p s (e d)"),
-                in_=Wv.rearrange("(s p e) d -> p s (e d)", s=4, p=P, e=2),
-            )
-            wv["raw"] = wr
-
-        def prep_wv():
-            wr = wv["raw"]
-            wg = const.tile([P, 2, DV, 2, 2], BF16, name="wv_grp", align_bytes=64)
-            for g in range(2):
-                nc.vector.tensor_copy(
-                    out=wg[:, g],
-                    in_=wr[:, 2 * g : 2 * g + 2].rearrange("p u e d -> p d u e"),
-                )
-            wc = const.tile([P, 2 * DV], U32, name="wv_c", align_bytes=64)
-            ws = const.tile([P, 2 * DV], U8, name="wv_s", align_bytes=64)
-            nc.vector.quantize_mx(
-                out=wc[:].bitcast(FP8X4),
-                scales=ws[:],
-                in_=wg[:].rearrange("p g d u e -> p (g d u e)"),
-            )
-            wv["c"] = wc
-            wv["s"] = ws
-            charge("v", 1500)
-
         def load_q(b):
-            qr = qp.tile([P, C], BF16, name="qraw", tag="qraw", bufs=4)
-            nc.sync.dma_start(out=qr[:], in_=q[b])
-            qraw[b] = qr
+            q_raw[b] = qp.tile([P, C], BF16, name="qraw", tag="qraw", bufs=B)
+            nc.sync.dma_start(out=q_raw[b][:], in_=q[b])
+
+        def load_wv():
+            wv["raw"] = const.tile([P, WCOLS, 2, DV], BF16, name="wv_raw")
+            nc.sync.dma_start(
+                out=wv["raw"][:].rearrange("p w e d -> p w (e d)"),
+                in_=Wv.rearrange("(w p e) d -> p w (e d)", w=WCOLS, p=P, e=2),
+            )
 
         def load(i):
-            kind, b, s, h = order[i]
+            kind, b, stream, h = halves[i]
             if i == 0:
                 load_q(0)
-            r = rawp.tile([P, 4, C], BF16, name="raw", tag="raw")
-            src = srcs[(kind, s)][b].rearrange("(p t) c -> p t c", t=8)
+            raw[i] = rawp.tile([P, TILES, C], BF16, name="raw", tag="raw")
+            rows = dram[(kind, stream)][b].rearrange("(m r) c -> m r c", r=2 * TILES)
             if i == 0:
-                for t in range(4):
-                    nc.sync.dma_start(out=r[:, t, :], in_=src[:, t, :])
+                for t in range(TILES):
+                    nc.sync.dma_start(out=raw[i][:, t, :], in_=rows[:, t, :])
             else:
-                nc.sync.dma_start(out=r[:], in_=src[:, 4 * h : 4 * h + 4, :])
-            raw[i] = r
-            if kind == "K" and s == 0 and h == 0 and b + 1 < B:
+                nc.sync.dma_start(out=raw[i][:], in_=rows[:, TILES * h : TILES * (h + 1), :])
+            if kind == "key" and stream == 0 and h == 0 and b + 1 < B:
                 load_q(b + 1)
-            if i == 9:
+            if i == KEY_STEPS // 2 + 1:
                 load_wv()
 
-        def q_transpose(b):
-            w = work_bank([P, 4, P], "wq")
-            qf = qraw[b][:].bitcast(F32)
-            for u in range(4):
-                nc.tensor.transpose(w[:, u, :], qf[:, P * u : P * (u + 1)], ident[:])
-            t = qp.tile([P, 4, 2, P], BF16, name="qT", tag="qT")
-            nc.vector.tensor_copy(
-                out=t[:],
-                in_=w[:].bitcast(BF16).rearrange("p u (n e) -> p u e n", e=2),
+        def quantise_wv():
+            side = const.tile([P, 2, DV, 2, 2], BF16, name="wv_grp", align_bytes=64)
+            for g in range(2):
+                nc.vector.tensor_copy(
+                    out=side[:, g],
+                    in_=wv["raw"][:, 2 * g : 2 * g + 2].rearrange("p u e d -> p d u e"),
+                )
+            wv["codes"] = const.tile([P, 2 * DV], U32, name="wv_c", align_bytes=64)
+            wv["scales"] = const.tile([P, 2 * DV], U8, name="wv_s", align_bytes=64)
+            nc.vector.quantize_mx(
+                out=wv["codes"][:].bitcast(FP8X4),
+                scales=wv["scales"][:],
+                in_=side[:].rearrange("p g d u e -> p (g d u e)"),
             )
-            charge("v", 1024)
-            qT[b] = t
 
-        def score_mms(job):
-            kind, b, s, h = order[job]
-            acc = score_bank()
-            sps[(b, s, h)] = acc
-            kb = kT[job][:].bitcast(BF16).rearrange("p u (n e) -> p u n e", e=2)
-            return [(acc, qT[b], kb, u, e) for u in range(4) for e in range(2)]
+        def transpose_q(b):
+            bank = work_bank([P, WCOLS, P], "wq")
+            words = q_raw[b][:].bitcast(F32)
+            for w in range(WCOLS):
+                nc.tensor.transpose(bank[:, w, :], words[:, P * w : P * (w + 1)], ident[:])
+            q_t[b] = qp.tile([P, WCOLS, 2, P], BF16, name="qT", tag="qT")
+            nc.vector.tensor_copy(
+                out=q_t[b][:],
+                in_=bank[:].bitcast(BF16).rearrange("p w (m e) -> p w e m", e=2),
+            )
 
-        def next_mm(mms):
-            if st["mm"] < len(mms):
-                acc, qt, kb, u, e = mms[st["mm"]]
-                st["mm"] += 1
-                nc.tensor.matmul(
-                    out=acc[:],
-                    lhsT=qt[:, u, e, :],
-                    rhs=kb[:, u, :, e],
-                    start=(u == 0 and e == 0),
-                    stop=(u == 3 and e == 1),
-                )
+        def score_matmuls(j):
+            kind, b, stream, h = halves[j]
+            score[(b, stream, h)] = score_bank()
+            keys = k_t[j][:].bitcast(BF16).rearrange("p w (m e) -> p w m e", e=2)
+            return [
+                (score[(b, stream, h)], q_t[b], keys, w, e) for w in range(WCOLS) for e in range(2)
+            ]
 
-        def transposes(i, mms, hook, last):
-            kind, b, s, h = order[i]
-            rf = raw[i][:].bitcast(F32)
-            if kind == "K":
-                dst = ktp.tile([P, 4, 512], F32, name="kT", tag="kT")
-                kT[i] = dst
+        def issue(matmul):
+            acc, queries, keys, w, e = matmul
+            nc.tensor.matmul(
+                out=acc[:],
+                lhsT=queries[:, w, e, :],
+                rhs=keys[:, w, :, e],
+                start=(w == 0 and e == 0),
+                stop=(w == WCOLS - 1 and e == 1),
+            )
+
+        def transposes(i, matmuls, stream_due):
+            kind, b, stream, h = halves[i]
+            words = raw[i][:].bitcast(F32)
+            if kind == "key":
+                k_t[i] = ktp.tile([P, WCOLS, HALF], F32, name="kT", tag="kT")
             else:
-                dst = grpp.tile([P, 4 * C], BF16, name="grp", tag="grp", align_bytes=64)
-                grp[i] = dst
-                dstf = dst[:].bitcast(F32).rearrange(
-                    "p (t g n u) -> p t g n u", t=4, g=2, n=P, u=2
+                grouped[i] = grpp.tile([P, TILES * C], BF16, name="grp", tag="grp", align_bytes=64)
+                side = grouped[i][:].bitcast(F32).rearrange(
+                    "p (t g m u) -> p t g m u", t=TILES, g=2, m=P, u=2
                 )
-            for t in range(4):
-                w = work_bank([P, 4, P], "wt")
-                for u in range(4):
-                    if WEAVE and u == 0:
-                        next_mm(mms)
-                        next_mm(mms)
-                    nc.tensor.transpose(
-                        w[:, u, :], rf[:, t, P * u : P * (u + 1)], ident[:]
-                    )
-                if hook and t == 0:
-                    st["s"] = min(st["s"], st["v"] - 1)
-                if kind == "K":
-                    copy_out(dst[:, :, P * t : P * (t + 1)], w[:])
+            for t in range(TILES):
+                bank = work_bank([P, WCOLS, P], "wt")
+                for w in range(WCOLS):
+                    if matmuls and w % 2 == 0:
+                        issue(matmuls[(WCOLS * t + w) // 2])
+                    nc.tensor.transpose(bank[:, w, :], words[:, t, P * w : P * (w + 1)], ident[:])
+                if kind == "key":
+                    copy_out(i, t, k_t[i][:, :, P * t : P * (t + 1)], bank[:])
                 else:
-                    copy_out(
-                        dstf[:, t], w[:].rearrange("p (g u) n -> p g n u", g=2, u=2)
-                    )
-                if hook and t == 0:
-                    exps(hook[0], hook[1])
-                if last and t == 1:
+                    copy_out(i, t, side[:, t], bank[:].rearrange("p (g u) m -> p g m u", g=2, u=2))
+                if stream_due and t == 0:
+                    exponentials(stream_due[0], stream_due[1])
+                if i == STEPS - 1 and t == 1:
                     quantise(i, 0, 2)
 
         def quantise(i, part, parts):
             if part == 0:
-                cod[i] = codp.tile([P, C], U32, name="cod", tag="cod", align_bytes=64)
-                sca[i] = codp.tile([P, C], U8, name="sca", tag="sca", align_bytes=64)
-            w = C // parts
-            cs = slice(part * w, (part + 1) * w)
+                codes[i] = codp.tile([P, C], U32, name="cod", tag="cod", align_bytes=64)
+                scales[i] = codp.tile([P, C], U8, name="sca", tag="sca", align_bytes=64)
+            width = C // parts
+            cols = slice(part * width, (part + 1) * width)
             nc.vector.quantize_mx(
-                out=cod[i][:, cs].bitcast(FP8X4),
-                scales=sca[i][:, cs],
-                in_=grp[i][:, 4 * part * w : 4 * (part + 1) * w],
+                out=codes[i][:, cols].bitcast(FP8X4),
+                scales=scales[i][:, cols],
+                in_=grouped[i][:, 4 * part * width : 4 * (part + 1) * width],
             )
 
-        def rowmax(b, s, h):
+        def row_maximum(b, stream, h):
             if h == 0:
-                mx2[(b, s)] = stp.tile([P, 2], F32, name="mx2", tag="mx2")
+                row_max[(b, stream)] = stp.tile([P, 2], F32, name="mx2", tag="mx2")
             nc.vector.reduce_max(
-                out=mx2[(b, s)][:, h : h + 1], in_=sps[(b, s, h)][:], axis=AX.X
+                out=row_max[(b, stream)][:, h : h + 1], in_=score[(b, stream, h)][:], axis=AXIS.X
             )
 
-        def negmax(b, s):
-            m = mx2[(b, s)]
-            nbt = stp.tile([P, 1], F32, name="nb", tag="nb")
-            nbs[(b, s)] = nbt
+        def negative_maximum(b, stream):
+            neg_max[(b, stream)] = stp.tile([P, 1], F32, name="nb", tag="nb")
             nc.vector.tensor_scalar(
-                out=nbt[:],
-                in0=m[:, 0:1],
-                scalar1=m[:, 1:2],
+                out=neg_max[(b, stream)][:],
+                in0=row_max[(b, stream)][:, 0:1],
+                scalar1=row_max[(b, stream)][:, 1:2],
                 scalar2=-SCALE,
                 op0=ALU.max,
                 op1=ALU.mult,
             )
 
-        def exps(b, s):
-            nbt = nbs[(b, s)]
-            e = ep.tile([P, N], F32, name="e%d" % s, tag="e%d" % s)
-            zz = stp.tile([P, 2], F32, name="z2", tag="z2")
+        def exponentials(b, stream):
+            expo[(b, stream)] = ep.tile([P, N], F32, name="e%d" % stream, tag="e%d" % stream)
+            exp_sum[(b, stream)] = stp.tile([P, 2], F32, name="z2", tag="z2")
             for h in range(2):
                 nc.scalar.activation(
-                    out=e[:, 512 * h : 512 * (h + 1)],
-                    in_=sps[(b, s, h)][:],
-                    func=ACTF.Exp,
-                    bias=nbt[:, 0:1],
+                    out=expo[(b, stream)][:, HALF * h : HALF * (h + 1)],
+                    in_=score[(b, stream, h)][:],
+                    func=ACT.Exp,
+                    bias=neg_max[(b, stream)][:, 0:1],
                     scale=SCALE,
-                    accum_out=zz[:, h : h + 1],
+                    accum_out=exp_sum[(b, stream)][:, h : h + 1],
                 )
-            ee[(b, s)] = e
-            z2[(b, s)] = zz
 
-        def compare(b, j):
-            o = ep.tile([P, N], BF16, name="ind%d" % j, tag="ind%d" % j)
-            nc.vector.scalar_tensor_tensor(
-                out=o[:],
-                in0=ee[(b, 0)][:],
-                scalar=rz[(b, 0)][:, 0:1],
-                in1=ee[(b, 1)][:],
-                op0=ALU.mult,
-                op1=(ALU.is_ge if j == 0 else ALU.is_le),
-            )
-            ind[(b, j)] = o
-
-        def votes_a(b):
-            for s in range(2):
-                zz = z2[(b, s)]
-                z = stp.tile([P, 1], F32, name="z", tag="z")
+        def normalise(b):
+            for stream in range(2):
+                total = stp.tile([P, 1], F32, name="z", tag="z")
                 nc.vector.tensor_tensor(
-                    out=z[:], in0=zz[:, 0:1], in1=zz[:, 1:2], op=ALU.add
+                    out=total[:],
+                    in0=exp_sum[(b, stream)][:, 0:1],
+                    in1=exp_sum[(b, stream)][:, 1:2],
+                    op=ALU.add,
                 )
-                r = stp.tile([P, 1], F32, name="rz", tag="rz")
-                nc.vector.reciprocal(out=r[:], in_=z[:])
-                rz[(b, s)] = r
-            e1 = ee[(b, 1)]
+                inv_sum[(b, stream)] = stp.tile([P, 1], F32, name="rz", tag="rz")
+                nc.vector.reciprocal(out=inv_sum[(b, stream)][:], in_=total[:])
             nc.vector.tensor_scalar(
-                out=e1[:], in0=e1[:], scalar1=rz[(b, 1)][:, 0:1], scalar2=None, op0=ALU.mult
+                out=expo[(b, 1)][:],
+                in0=expo[(b, 1)][:],
+                scalar1=inv_sum[(b, 1)][:, 0:1],
+                scalar2=None,
+                op0=ALU.mult,
             )
-            compare(b, 0)
 
-        def counts(b):
-            w = work_bank([P, 8, 2, 2], "wc")
-            for t in range(8):
-                for j in range(2):
+        def compare(b, v):
+            vote[(b, v)] = ep.tile([P, N], BF16, name="ind%d" % v, tag="ind%d" % v)
+            nc.vector.scalar_tensor_tensor(
+                out=vote[(b, v)][:],
+                in0=expo[(b, 0)][:],
+                scalar=inv_sum[(b, 0)][:, 0:1],
+                in1=expo[(b, 1)][:],
+                op0=ALU.mult,
+                op1=(ALU.is_ge if v == 0 else ALU.is_le),
+            )
+
+        def count(b):
+            bank = work_bank([P, 2 * TILES, 2, 2], "wc")
+            for r in range(2 * TILES):
+                for v in range(2):
                     nc.tensor.matmul(
-                        out=w[:, t, j, :],
-                        lhsT=ind[(b, j)][:, P * t : P * (t + 1)],
-                        rhs=ones[:],
+                        out=bank[:, r, v, :],
+                        lhsT=vote[(b, v)][:, P * r : P * (r + 1)],
+                        rhs=share[:],
                         start=True,
                         stop=True,
                     )
-            a = abp.tile([P, 8, 2, 2], F32, name="ab", tag="ab")
-            nc.vector.tensor_copy(out=a[:], in_=w[:])
-            ab[b] = a
+            ratio[b] = abp.tile([P, 2 * TILES, 2, 2], F32, name="ab", tag="ab")
+            nc.vector.tensor_copy(out=ratio[b][:], in_=bank[:])
 
-        def mx_bank(i, j, fine):
-            kind, b, s, h = order[i]
-            if j == 0:
-                if s == 0:
-                    tmp[(b, h)] = outp.tile([P, 4, DV], F32, name="tmp", tag="tmp")
+        def multiply(i, pair, store_tiles):
+            kind, b, stream, h = halves[i]
+            if pair == 0 and stream == 0:
+                first_mix[(b, h)] = outp.tile([P, TILES, DV], F32, name="tmp", tag="tmp")
+            if pair == 0 and stream == 1:
+                mixed[(b, h)] = outp.tile([P, TILES, DV], F32, name="osb", tag="osb")
+            rows = out[b].rearrange("(m r) d -> m r d", r=2 * TILES)
+            bank = work_bank([P, 2, DV], "wv")
+            for t in (2 * pair, 2 * pair + 1):
+                for g in range(2):
+                    cols = slice((2 * t + g) * P, (2 * t + g + 1) * P)
+                    wv_cols = slice(g * DV, (g + 1) * DV)
+                    nc.tensor.matmul_mx(
+                        out=bank[:, t % 2, :],
+                        lhsT=codes[i][:, cols].bitcast(FP8X4),
+                        lhsT_scale=scales[i][:, cols],
+                        rhs=wv["codes"][:, wv_cols].bitcast(FP8X4),
+                        rhs_scale=wv["scales"][:, wv_cols],
+                        start=(g == 0),
+                        stop=(g == 1),
+                    )
+            for t in (2 * pair, 2 * pair + 1):
+                r = TILES * h + t
+                if stream == 0:
+                    nc.scalar.activation(
+                        out=first_mix[(b, h)][:, t, :],
+                        in_=bank[:, t % 2, :],
+                        func=ACT.Copy,
+                        scale=ratio[b][:, r, 0, 0:1],
+                    )
                 else:
-                    osb[(b, h)] = outp.tile([P, 4, DV], F32, name="osb", tag="osb")
-            dst = tmp[(b, h)] if s == 0 else osb[(b, h)]
-            o = out[b].rearrange("(p t) d -> p t d", t=8)
-            if True:
-                w = work_bank([P, 2, DV], "wv")
-                for jj in range(2):
-                    t = 2 * j + jj
-                    for g in range(2):
-                        cs = slice((2 * t + g) * P, (2 * t + g + 1) * P)
-                        ws = slice(g * DV, (g + 1) * DV)
-                        nc.tensor.matmul_mx(
-                            out=w[:, jj, :],
-                            lhsT=cod[i][:, cs].bitcast(FP8X4),
-                            lhsT_scale=sca[i][:, cs],
-                            rhs=wv["c"][:, ws].bitcast(FP8X4),
-                            rhs_scale=wv["s"][:, ws],
-                            start=(g == 0),
-                            stop=(g == 1),
-                        )
-                for jj in range(2):
-                    t = 2 * j + jj
-                    gt = 4 * h + t
-                    if s == 0:
-                        nc.scalar.activation(
-                            out=dst[:, t, :],
-                            in_=w[:, jj, :],
-                            func=ACTF.Copy,
-                            scale=ab[b][:, gt, 0, 0:1],
-                        )
-                    else:
-                        nc.vector.scalar_tensor_tensor(
-                            out=dst[:, t, :],
-                            in0=w[:, jj, :],
-                            scalar=ab[b][:, gt, 1, 0:1],
-                            in1=tmp[(b, h)][:, t, :],
-                            op0=ALU.mult,
-                            op1=ALU.add,
-                        )
-                        if fine:
-                            nc.sync.dma_start(out=o[:, gt, :], in_=dst[:, t, :])
-            if s == 1 and j == 1 and not fine:
-                nc.sync.dma_start(out=o[:, 4 * h : 4 * h + 4, :], in_=dst[:])
-            if s == 1 and j == 0 and i == nstep - 1:
-                nc.sync.dma_start(out=o[:, 4 * h : 4 * h + 2, :], in_=dst[:, 0:2, :])
-
-        def mx_job(i):
-            mx_bank(i, 0, False)
-            mx_bank(i, 1, False)
+                    nc.vector.scalar_tensor_tensor(
+                        out=mixed[(b, h)][:, t, :],
+                        in0=bank[:, t % 2, :],
+                        scalar=ratio[b][:, r, 1, 0:1],
+                        in1=first_mix[(b, h)][:, t, :],
+                        op0=ALU.mult,
+                        op1=ALU.add,
+                    )
+                    if store_tiles:
+                        nc.sync.dma_start(out=rows[:, r, :], in_=mixed[(b, h)][:, t, :])
+            if stream == 1 and pair == 1 and not store_tiles:
+                nc.sync.dma_start(
+                    out=rows[:, TILES * h : TILES * (h + 1), :], in_=mixed[(b, h)][:]
+                )
 
         for i in range(AHEAD):
             load(i)
-        q_transpose(0)
-        for i in range(nstep):
-            if i + AHEAD < nstep:
+        transpose_q(0)
+        for i in range(STEPS):
+            if i + AHEAD < STEPS:
                 load(i + AHEAD)
-            if i == 19:
-                st["nwork"] = 8
-                st["wb"] = 0
-            jq = i - 1
-            jr = i - 3
-            jm = i - 2
-            if NK <= jq < nstep:
-                charge("v", 1024)
-            if 0 <= jr < NK:
-                charge("v", 512)
-                if jr % 2 == 1:
-                    charge("v", 0)
-                    charge("s", 2 * 512 + 2 * FIX)
-            if 0 <= i - 7 < NK and (i - 7) % 4 == 0:
-                charge("v", 512 + 1024 + 6 * FIX)
-            if 0 <= i - 9 < NK and (i - 9) % 4 == 0:
-                charge("v", 1024)
-            if NK <= jm < nstep:
-                charge("s" if order[jm][2] == 0 else "v", 4 * (DV + FIX))
+            if i == LAST_SCORE_STEP + 1:
+                turn["work_banks"] = ALL_BANKS
+                turn["work"] = 0
 
-            hook = None
-            if 0 <= jr < NK:
-                kind, b, s, h = order[jr]
-                rowmax(b, s, h)
+            stream_due = None
+            j = i - MAX_LAG
+            if 0 <= j < KEY_STEPS:
+                kind, b, stream, h = halves[j]
+                row_maximum(b, stream, h)
                 if h == 1:
-                    negmax(b, s)
-                    hook = (b, s)
-            if i == 12:
-                prep_wv()
-            if NK <= jq < nstep:
-                quantise(jq, 0, 1)
-            if 0 <= i - 7 < NK and (i - 7) % 4 == 0:
-                votes_a((i - 7) // 4)
-            if 0 <= i - 9 < NK and (i - 9) % 4 == 0:
-                compare((i - 9) // 4, 1)
-            mms = []
-            st["mm"] = 0
-            if 0 <= i - 2 < NK:
-                mms = score_mms(i - 2)
-            if not WEAVE:
-                while st["mm"] < len(mms):
-                    next_mm(mms)
-            if i < nstep:
-                transposes(i, mms, hook, i == nstep - 1)
-            while st["mm"] < len(mms):
-                next_mm(mms)
-            if i < NK and i % 4 == 1 and i // 4 + 1 < B:
-                q_transpose(i // 4 + 1)
-            if 0 <= i - 10 < NK and (i - 10) % 4 == 0:
-                counts((i - 10) // 4)
-            if NK <= jm < nstep and i < nstep - 1:
-                mx_job(jm)
-        mx_bank(nstep - 3, 0, False)
-        quantise(nstep - 1, 1, 2)
-        mx_bank(nstep - 3, 1, False)
-        mx_job(nstep - 2)
-        mx_bank(nstep - 1, 0, False)
-        mx_bank(nstep - 1, 1, True)
+                    negative_maximum(b, stream)
+                    stream_due = (b, stream)
+            if i == KEY_STEPS - PER_BATCH:
+                quantise_wv()
+            if KEY_STEPS <= i - QUANT_LAG:
+                quantise(i - QUANT_LAG, 0, 1)
+            if batch_due(i, GE_LAG) is not None:
+                normalise(batch_due(i, GE_LAG))
+                compare(batch_due(i, GE_LAG), 0)
+            if batch_due(i, LE_LAG) is not None:
+                compare(batch_due(i, LE_LAG), 1)
+
+            matmuls = []
+            if 0 <= i - SCORE_LAG < KEY_STEPS:
+                matmuls = score_matmuls(i - SCORE_LAG)
+            transposes(i, matmuls, stream_due)
+            if i < KEY_STEPS and i % PER_BATCH == 1 and i // PER_BATCH + 1 < B:
+                transpose_q(i // PER_BATCH + 1)
+            if batch_due(i, COUNT_LAG) is not None:
+                count(batch_due(i, COUNT_LAG))
+            if KEY_STEPS <= i - MX_LAG and i < STEPS - 1:
+                multiply(i - MX_LAG, 0, False)
+                multiply(i - MX_LAG, 1, False)
+
+        multiply(STEPS - 3, 0, False)
+        quantise(STEPS - 1, 1, 2)
+        multiply(STEPS - 3, 1, False)
+        multiply(STEPS - 2, 0, False)
+        multiply(STEPS - 2, 1, False)
+        multiply(STEPS - 1, 0, True)
+        multiply(STEPS - 1, 1, True)

@@ -86,19 +86,8 @@ def tile_crossattention_for_fusion_temporal_pa_t_kernel(tc, q, k, ki, xs, xis, W
                 return j // PER_BATCH
             return None
 
-        def second_mix_due(i):
-            j = i - MX_LAG
-            return KEY_STEPS <= j < STEPS and halves[j][2] == 1
-
-        def vector_is_taken(i):
-            return (
-                batch_due(i, GE_LAG) is not None
-                or batch_due(i, LE_LAG) is not None
-                or second_mix_due(i)
-            )
-
         def copy_out(i, t, dst, src):
-            if t % 2 == 1 and not vector_is_taken(i):
+            if i % 2 == 0 and t % 2 == 1:
                 nc.vector.tensor_copy(out=dst, in_=src)
             else:
                 nc.scalar.copy(out=dst, in_=src)

from contextlib import ExitStack

import concourse.masks as masks
import concourse.mybir as mybir

F32 = mybir.dt.float32
BF16 = mybir.dt.bfloat16
U32 = mybir.dt.uint32
U8 = mybir.dt.uint8
FP8X4 = mybir.dt.float8_e4m3fn_x4
ALU = mybir.AluOpType
ACT = mybir.ActivationFunctionType
AXIS = mybir.AxisListType

B, NT, N, C, DV = 4, 128, 1024, 1024, 256
P = 128
HALF = N // 2
TILES = HALF // P
WCOLS = C // (2 * P)
FLOPS = 2 * 2 * B * NT * N * C + 2 * 2 * B * N * C * DV
SCALE = 1.0 / 32.0

PER_BATCH = 4
KEY_STEPS = PER_BATCH * B
STEPS = 2 * KEY_STEPS
RAW_BUFS = 8
AHEAD = RAW_BUFS - 1

SCORE_LAG = 2
MAX_LAG = 3
QUANT_LAG = 1
MX_LAG = 2
GE_LAG = 4
LE_LAG = 6
COUNT_LAG = 7

SCORE_BANKS = 3
WORK_BANKS = 5
ALL_BANKS = 8
LAST_SCORE_STEP = KEY_STEPS - 1 + MAX_LAG


def tile_crossattention_for_fusion_temporal_pa_t_kernel(tc, q, k, ki, xs, xis, Wv, out):
    nc = tc.nc
    with ExitStack() as ctx:
        ctx.enter_context(tc.manual_schedule())
        const = ctx.enter_context(tc.tile_pool(name="const", bufs=1))
        rawp = ctx.enter_context(tc.tile_pool(name="rawp", bufs=RAW_BUFS))
        qp = ctx.enter_context(tc.tile_pool(name="qp", bufs=2))
        ktp = ctx.enter_context(tc.tile_pool(name="ktp", bufs=4))
        grpp = ctx.enter_context(tc.tile_pool(name="grpp", bufs=3))
        codp = ctx.enter_context(tc.tile_pool(name="codp", bufs=4))
        ep = ctx.enter_context(tc.tile_pool(name="ep", bufs=2))
        stp = ctx.enter_context(tc.tile_pool(name="stp", bufs=4))
        abp = ctx.enter_context(tc.tile_pool(name="abp", bufs=B))
        outp = ctx.enter_context(tc.tile_pool(name="outp", bufs=3))
        psum = ctx.enter_context(tc.psum_pool(name="psum", bufs=1))

        ident = const.tile([P, P], F32, name="ident")
        masks.make_identity(nc, ident[:])
        share = const.tile([P, 2], BF16, name="share")
        nc.vector.memset(share[:], 1.0 / NT)

        halves = [("key", b, stream, h) for b in range(B) for stream in range(2) for h in range(2)]
        halves += [("val", b, stream, h) for b in range(B) for h in range(2) for stream in range(2)]
        dram = {("key", 0): k, ("key", 1): ki, ("val", 0): xs, ("val", 1): xis}

        raw, q_raw, q_t, k_t, grouped, codes, scales = {}, {}, {}, {}, {}, {}, {}
        score, row_max, neg_max, expo, exp_sum, inv_sum, vote, ratio = {}, {}, {}, {}, {}, {}, {}, {}
        first_mix, mixed, wv = {}, {}, {}
        turn = {"work": 0, "work_banks": WORK_BANKS, "score": 0}

        def work_bank(shape, name):
            bank = turn["work"] % turn["work_banks"]
            turn["work"] += 1
            return psum.tile(shape, F32, name=name, tag="bank%d" % bank)

        def score_bank():
            bank = WORK_BANKS + turn["score"] % SCORE_BANKS
            turn["score"] += 1
            return psum.tile([P, HALF], F32, name="sacc", tag="bank%d" % bank)

        def batch_due(i, lag):
            j = i - lag
            if 0 <= j < KEY_STEPS and j % PER_BATCH == PER_BATCH - 1:
                return j // PER_BATCH
            return None

        def copy_out(i, t, dst, src):
            if i % 2 == 0 and t % 2 == 1:
                nc.vector.tensor_copy(out=dst, in_=src)
            else:
                nc.scalar.copy(out=dst, in_=src)

        def load_q(b):
            q_raw[b] = qp.tile([P, C], BF16, name="qraw", tag="qraw", bufs=B)
            nc.sync.dma_start(out=q_raw[b][:], in_=q[b])

        def load_wv():
            wv["raw"] = const.tile([P, WCOLS, 2, DV], BF16, name="wv_raw")
            nc.sync.dma_start(
                out=wv["raw"][:].rearrange("p w e d -> p w (e d)"),
                in_=Wv.rearrange("(w p e) d -> p w (e d)", w=WCOLS, p=P, e=2),
            )

        def load(i):
            kind, b, stream, h = halves[i]
            if i == 0:
                load_q(0)
            raw[i] = rawp.tile([P, TILES, C], BF16, name="raw", tag="raw")
            rows = dram[(kind, stream)][b].rearrange("(m r) c -> m r c", r=2 * TILES)
            if i == 0:
                for t in range(TILES):
                    nc.sync.dma_start(out=raw[i][:, t, :], in_=rows[:, t, :])
            else:
                nc.sync.dma_start(out=raw[i][:], in_=rows[:, TILES * h : TILES * (h + 1), :])
            if kind == "key" and stream == 0 and h == 0 and b + 1 < B:
                load_q(b + 1)
            if i == KEY_STEPS // 2 + 1:
                load_wv()

        def quantise_wv():
            side = const.tile([P, 2, DV, 2, 2], BF16, name="wv_grp", align_bytes=64)
            for g in range(2):
                nc.vector.tensor_copy(
                    out=side[:, g],
                    in_=wv["raw"][:, 2 * g : 2 * g + 2].rearrange("p u e d -> p d u e"),
                )
            wv["codes"] = const.tile([P, 2 * DV], U32, name="wv_c", align_bytes=64)
            wv["scales"] = const.tile([P, 2 * DV], U8, name="wv_s", align_bytes=64)
            nc.vector.quantize_mx(
                out=wv["codes"][:].bitcast(FP8X4),
                scales=wv["scales"][:],
                in_=side[:].rearrange("p g d u e -> p (g d u e)"),
            )

        def transpose_q(b):
            bank = work_bank([P, WCOLS, P], "wq")
            words = q_raw[b][:].bitcast(F32)
            for w in range(WCOLS):
                nc.tensor.transpose(bank[:, w, :], words[:, P * w : P * (w + 1)], ident[:])
            q_t[b] = qp.tile([P, WCOLS, 2, P], BF16, name="qT", tag="qT")
            nc.vector.tensor_copy(
                out=q_t[b][:],
                in_=bank[:].bitcast(BF16).rearrange("p w (m e) -> p w e m", e=2),
            )

        def score_matmuls(j):
            kind, b, stream, h = halves[j]
            score[(b, stream, h)] = score_bank()
            keys = k_t[j][:].bitcast(BF16).rearrange("p w (m e) -> p w m e", e=2)
            return [
                (score[(b, stream, h)], q_t[b], keys, w, e) for w in range(WCOLS) for e in range(2)
            ]

        def issue(matmul):
            acc, queries, keys, w, e = matmul
            nc.tensor.matmul(
                out=acc[:],
                lhsT=queries[:, w, e, :],
                rhs=keys[:, w, :, e],
                start=(w == 0 and e == 0),
                stop=(w == WCOLS - 1 and e == 1),
            )

        def transposes(i, matmuls, stream_due):
            kind, b, stream, h = halves[i]
            words = raw[i][:].bitcast(F32)
            if kind == "key":
                k_t[i] = ktp.tile([P, WCOLS, HALF], F32, name="kT", tag="kT")
            else:
                grouped[i] = grpp.tile([P, TILES * C], BF16, name="grp", tag="grp", align_bytes=64)
                side = grouped[i][:].bitcast(F32).rearrange(
                    "p (t g m u) -> p t g m u", t=TILES, g=2, m=P, u=2
                )
            for t in range(TILES):
                bank = work_bank([P, WCOLS, P], "wt")
                for w in range(WCOLS):
                    if matmuls and w % 2 == 0:
                        issue(matmuls[(WCOLS * t + w) // 2])
                    nc.tensor.transpose(bank[:, w, :], words[:, t, P * w : P * (w + 1)], ident[:])
                if kind == "key":
                    copy_out(i, t, k_t[i][:, :, P * t : P * (t + 1)], bank[:])
                else:
                    copy_out(i, t, side[:, t], bank[:].rearrange("p (g u) m -> p g m u", g=2, u=2))
                if stream_due and t == 0:
                    exponentials(stream_due[0], stream_due[1])
                if i == STEPS - 1 and t == 1:
                    quantise(i, 0, 2)

        def quantise(i, part, parts):
            if part == 0:
                codes[i] = codp.tile([P, C], U32, name="cod", tag="cod", align_bytes=64)
                scales[i] = codp.tile([P, C], U8, name="sca", tag="sca", align_bytes=64)
            width = C // parts
            cols = slice(part * width, (part + 1) * width)
            nc.vector.quantize_mx(
                out=codes[i][:, cols].bitcast(FP8X4),
                scales=scales[i][:, cols],
                in_=grouped[i][:, 4 * part * width : 4 * (part + 1) * width],
            )

        def row_maximum(b, stream, h):
            if h == 0:
                row_max[(b, stream)] = stp.tile([P, 2], F32, name="mx2", tag="mx2")
            nc.vector.reduce_max(
                out=row_max[(b, stream)][:, h : h + 1], in_=score[(b, stream, h)][:], axis=AXIS.X
            )

        def negative_maximum(b, stream):
            neg_max[(b, stream)] = stp.tile([P, 1], F32, name="nb", tag="nb")
            nc.vector.tensor_scalar(
                out=neg_max[(b, stream)][:],
                in0=row_max[(b, stream)][:, 0:1],
                scalar1=row_max[(b, stream)][:, 1:2],
                scalar2=-SCALE,
                op0=ALU.max,
                op1=ALU.mult,
            )

        def exponentials(b, stream):
            expo[(b, stream)] = ep.tile([P, N], F32, name="e%d" % stream, tag="e%d" % stream)
            exp_sum[(b, stream)] = stp.tile([P, 2], F32, name="z2", tag="z2")
            for h in range(2):
                nc.scalar.activation(
                    out=expo[(b, stream)][:, HALF * h : HALF * (h + 1)],
                    in_=score[(b, stream, h)][:],
                    func=ACT.Exp,
                    bias=neg_max[(b, stream)][:, 0:1],
                    scale=SCALE,
                    accum_out=exp_sum[(b, stream)][:, h : h + 1],
                )

        def normalise(b):
            for stream in range(2):
                total = stp.tile([P, 1], F32, name="z", tag="z")
                nc.vector.tensor_tensor(
                    out=total[:],
                    in0=exp_sum[(b, stream)][:, 0:1],
                    in1=exp_sum[(b, stream)][:, 1:2],
                    op=ALU.add,
                )
                inv_sum[(b, stream)] = stp.tile([P, 1], F32, name="rz", tag="rz")
                nc.vector.reciprocal(out=inv_sum[(b, stream)][:], in_=total[:])
            nc.vector.tensor_scalar(
                out=expo[(b, 1)][:],
                in0=expo[(b, 1)][:],
                scalar1=inv_sum[(b, 1)][:, 0:1],
                scalar2=None,
                op0=ALU.mult,
            )

        def compare(b, v):
            vote[(b, v)] = ep.tile([P, N], BF16, name="ind%d" % v, tag="ind%d" % v)
            nc.vector.scalar_tensor_tensor(
                out=vote[(b, v)][:],
                in0=expo[(b, 0)][:],
                scalar=inv_sum[(b, 0)][:, 0:1],
                in1=expo[(b, 1)][:],
                op0=ALU.mult,
                op1=(ALU.is_ge if v == 0 else ALU.is_le),
            )

        def count(b):
            bank = work_bank([P, 2 * TILES, 2, 2], "wc")
            for r in range(2 * TILES):
                for v in range(2):
                    nc.tensor.matmul(
                        out=bank[:, r, v, :],
                        lhsT=vote[(b, v)][:, P * r : P * (r + 1)],
                        rhs=share[:],
                        start=True,
                        stop=True,
                    )
            ratio[b] = abp.tile([P, 2 * TILES, 2, 2], F32, name="ab", tag="ab")
            nc.vector.tensor_copy(out=ratio[b][:], in_=bank[:])

        def multiply(i, pair, store_tiles):
            kind, b, stream, h = halves[i]
            if pair == 0 and stream == 0:
                first_mix[(b, h)] = outp.tile([P, TILES, DV], F32, name="tmp", tag="tmp")
            if pair == 0 and stream == 1:
                mixed[(b, h)] = outp.tile([P, TILES, DV], F32, name="osb", tag="osb")
            rows = out[b].rearrange("(m r) d -> m r d", r=2 * TILES)
            bank = work_bank([P, 2, DV], "wv")
            for t in (2 * pair, 2 * pair + 1):
                for g in range(2):
                    cols = slice((2 * t + g) * P, (2 * t + g + 1) * P)
                    wv_cols = slice(g * DV, (g + 1) * DV)
                    nc.tensor.matmul_mx(
                        out=bank[:, t % 2, :],
                        lhsT=codes[i][:, cols].bitcast(FP8X4),
                        lhsT_scale=scales[i][:, cols],
                        rhs=wv["codes"][:, wv_cols].bitcast(FP8X4),
                        rhs_scale=wv["scales"][:, wv_cols],
                        start=(g == 0),
                        stop=(g == 1),
                    )
            for t in (2 * pair, 2 * pair + 1):
                r = TILES * h + t
                if stream == 0:
                    nc.scalar.activation(
                        out=first_mix[(b, h)][:, t, :],
                        in_=bank[:, t % 2, :],
                        func=ACT.Copy,
                        scale=ratio[b][:, r, 0, 0:1],
                    )
                else:
                    nc.vector.scalar_tensor_tensor(
                        out=mixed[(b, h)][:, t, :],
                        in0=bank[:, t % 2, :],
                        scalar=ratio[b][:, r, 1, 0:1],
                        in1=first_mix[(b, h)][:, t, :],
                        op0=ALU.mult,
                        op1=ALU.add,
                    )
                    if store_tiles:
                        nc.sync.dma_start(out=rows[:, r, :], in_=mixed[(b, h)][:, t, :])
            if stream == 1 and pair == 1 and not store_tiles:
                nc.sync.dma_start(
                    out=rows[:, TILES * h : TILES * (h + 1), :], in_=mixed[(b, h)][:]
                )

        for i in range(AHEAD):
            load(i)
        transpose_q(0)
        for i in range(STEPS):
            if i + AHEAD < STEPS:
                load(i + AHEAD)
            if i == LAST_SCORE_STEP + 1:
                turn["work_banks"] = ALL_BANKS
                turn["work"] = 0

            stream_due = None
            j = i - MAX_LAG
            if 0 <= j < KEY_STEPS:
                kind, b, stream, h = halves[j]
                row_maximum(b, stream, h)
                if h == 1:
                    negative_maximum(b, stream)
                    stream_due = (b, stream)
            if i == KEY_STEPS - PER_BATCH:
                quantise_wv()
            if KEY_STEPS <= i - QUANT_LAG:
                quantise(i - QUANT_LAG, 0, 1)
            if batch_due(i, GE_LAG) is not None:
                normalise(batch_due(i, GE_LAG))
                compare(batch_due(i, GE_LAG), 0)
            if batch_due(i, LE_LAG) is not None:
                compare(batch_due(i, LE_LAG), 1)

            matmuls = []
            if 0 <= i - SCORE_LAG < KEY_STEPS:
                matmuls = score_matmuls(i - SCORE_LAG)
            transposes(i, matmuls, stream_due)
            if i < KEY_STEPS and i % PER_BATCH == 1 and i // PER_BATCH + 1 < B:
                transpose_q(i // PER_BATCH + 1)
            if batch_due(i, COUNT_LAG) is not None:
                count(batch_due(i, COUNT_LAG))
            if KEY_STEPS <= i - MX_LAG and i < STEPS - 1:
                multiply(i - MX_LAG, 0, False)
                multiply(i - MX_LAG, 1, False)

        multiply(STEPS - 3, 0, False)
        quantise(STEPS - 1, 1, 2)
        multiply(STEPS - 3, 1, False)
        multiply(STEPS - 2, 0, False)
        multiply(STEPS - 2, 1, False)
        multiply(STEPS - 1, 0, True)
        multiply(STEPS - 1, 1, True)
